import numpy as np
import ml_dtypes


def mxq(x, axis, fmt="e4m3"):
    dtype, down = {"e4m3": (ml_dtypes.float8_e4m3fn, 7), "e5m2": (ml_dtypes.float8_e5m2, 14)}[fmt]
    v = np.moveaxis(np.asarray(x, np.float32).astype(ml_dtypes.bfloat16).astype(np.float64), axis, -1)
    blocks = v.reshape(v.shape[:-1] + (-1, 32))
    amax = np.abs(blocks).max(-1, keepdims=True)
    byte = np.maximum(np.where(amax > 0, np.frexp(amax)[1] - 1 + 127, 0) - down, 1)
    scale = np.exp2(byte - 127.0)
    codes = (blocks / scale).astype(np.float32).astype(dtype).astype(np.float64)
    return np.moveaxis((codes * scale).reshape(v.shape), -1, axis)


WIDE = False


def mx_kscale(k):
    if not WIDE:
        return np.ones(k)
    levels = np.array([10, -10, 5, -5, 0])
    a = np.random.permutation(np.resize(levels, k // 512 * 4)).reshape(k // 512, 4)
    idx = np.arange(k)
    return np.exp2(a[idx // 512, idx % 128 // 32])


BF16 = ml_dtypes.bfloat16


def bf(x):
    return np.asarray(x, np.float32).astype(BF16)


def f64(x):
    return np.asarray(x).astype(np.float64)


B, L, D, E, S, H = 4, 512, 512, 16, 32, 1024
K = E * S


def softmax(v):
    e = np.exp(v - v.max(-1, keepdims=True))
    return e / e.sum(-1, keepdims=True)


def setup_inputs():
    s = mx_kscale(H)
    return {"h": bf(np.random.standard_normal((B, E, S, H)) * 0.6 * s),
            "w2": bf(np.random.standard_normal((E, H, D)) * 1.5 / np.sqrt(H) / s[:, None]),
            "b2": bf(np.random.standard_normal((E, D)) * 0.5),
            "logits": bf(np.random.standard_normal((B, L, E, S)) * 2.0)}


def reference(h, w2, b2, logits):
    eo = (mxq(f64(h), 3, "e4m3") @ mxq(f64(w2), 1, "e4m3")) + f64(b2)[:, None, :]
    eo = eo.reshape(B, K, D)
    c_w = softmax(f64(logits).reshape(B, L, K))
    return mxq(c_w, 2, "e4m3") @ mxq(eo, 1, "e4m3")

@@ -1,0 +1,344 @@
+from contextlib import ExitStack
+
+import concourse.mybir as mybir
+from concourse.masks import make_identity
+
+F32 = mybir.dt.float32
+BF16 = mybir.dt.bfloat16
+U32 = mybir.dt.uint32
+U8 = mybir.dt.uint8
+FP8X4 = mybir.dt.float8_e4m3fn_x4
+ACT = mybir.ActivationFunctionType
+ALU = mybir.AluOpType
+AXIS = mybir.AxisListType
+
+P = 128
+NB, NL, ND, NE, NS, NH = 4, 512, 512, 16, 32, 1024
+FLOPS = 2 * NB * NE * NS * NH * ND + 2 * NB * NL * NE * NS * ND
+
+W_BUFS = 5
+N_UNITS = 2 * NE
+S_UNITS = (6, 9, 12, 15, 18, 21, 24, 27, 30)
+S_AHEAD = 3
+Q_LAG = 2
+LAST_SLOT = N_UNITS + Q_LAG + 1
+TPS_TAGS = ("tr", "tr", "ps1", "ps1", "cps", "cps", "tr", "tr")
+
+
+def tile_softmoe_pb_kernel(tc, h, w2, b2, logits, out):
+    nc = tc.nc
+    with ExitStack() as ctx:
+        const = ctx.enter_context(tc.tile_pool(name="const", bufs=1))
+        smpool = ctx.enter_context(tc.tile_pool(name="smpool", bufs=2))
+        epool = ctx.enter_context(tc.tile_pool(name="epool", bufs=4))
+        psum = ctx.enter_context(tc.psum_pool(name="psum", bufs=2))
+        ctx.enter_context(tc.manual_schedule())
+
+        ident_f = const.tile([P, P], F32, name="ident_f")
+        make_identity(nc, ident_f[:])
+        ident_b = const.tile([P, P], BF16, name="ident_b")
+        make_identity(nc, ident_b[:])
+
+        h_words = [const.tile([P, 1024], U32, name="h_words%d" % eg, align_bytes=64) for eg in range(4)]
+        h_scales = [const.tile([P, 1024], U8, name="h_scales%d" % eg, align_bytes=64) for eg in range(4)]
+        cw_words = [const.tile([P, NL], U32, name="cw_words%d" % b, align_bytes=64) for b in range(NB)]
+        cw_scales = [const.tile([P, NL], U8, name="cw_scales%d" % b, align_bytes=64) for b in range(NB)]
+        lraw = [const.tile([P, 4, 512], BF16, name="lraw%d" % b) for b in range(NB)]
+        eoT = const.tile([P, 4, NB, 512], BF16, name="eoT")
+        b2z = const.tile([P, ND], BF16, name="b2z")
+        b2T = const.tile([P, 4, NE], F32, name="b2T")
+
+        wtiles = {}
+        htiles = {}
+        state = {}
+
+        def load_w(e):
+            wraw = wpool.tile([P, 8, ND], BF16, name="wraw", tag="wraw")
+            src = w2[e].rearrange("(c p r) d -> p c (r d)", c=4, p=P, r=2)
+            dst = wraw[:].rearrange("p (c r) d -> p c (r d)", c=4, r=2)
+            if e == 0:
+                nc.sync.dma_start(out=dst[:, 0:2, :], in_=src[:, 0:2, :])
+                nc.sync.dma_start(out=dst[:, 2:4, :], in_=src[:, 2:4, :])
+            else:
+                nc.sync.dma_start(out=dst, in_=src)
+            wtiles[e] = wraw
+
+        def load_h(eg):
+            for b in range(NB):
+                hraw = hpool.tile([P, NH], BF16, name="hraw", tag="hraw")
+                nc.sync.dma_start(out=hraw[:], in_=h[b, 4 * eg:4 * eg + 4].rearrange("e s k -> (e s) k"))
+                htiles[(eg, b)] = hraw
+
+        def load_logits(b):
+            nc.sync.dma_start(out=lraw[b][:], in_=logits[b].rearrange("(p j) e s -> p j (e s)", j=4))
+
+        def h_tile(eg, b):
+            if b == 0:
+                state[("gh", eg)] = ghpool.tile([P, 4096], BF16, name="gh", tag="gh", align_bytes=64)
+            gh = state[("gh", eg)]
+            gh32 = gh[:].bitcast(F32).rearrange("p (a b s u) -> p a b s u", a=8, b=NB, s=NS, u=2)
+            hps = psum.tile([P, 2, 8, NS], F32, name="hps", tag="tr")
+            words = htiles[(eg, b)][:].bitcast(F32)
+            for g in range(2):
+                for u in range(2):
+                    c = 2 * g + u
+                    nc.tensor.transpose(
+                        hps[:, u, 4 * g:4 * g + 4, :].rearrange("p e s -> p (e s)"),
+                        words[:, c * P:(c + 1) * P],
+                        ident_f[:],
+                    )
+            nc.scalar.copy(out=gh32[:, :, b, :, :], in_=hps[:].rearrange("p u a s -> p a s u"))
+
+        def h_quant(eg):
+            nc.vector.quantize_mx(out=h_words[eg][:].bitcast(FP8X4), scales=h_scales[eg][:], in_=state[("gh", eg)][:])
+
+        def regroup_w(i):
+            e, g = divmod(i, 2)
+            wg = gpool.tile([P, ND, 4], BF16, name="wg", tag="wg", align_bytes=64)
+            dst = wg[:].rearrange("p (c i) t -> p c t i", i=4)
+            src = wtiles[e][:, 4 * g:4 * g + 4, :].rearrange("p t (c i) -> p c t i", i=4)
+            if i in S_UNITS:
+                nc.scalar.copy(out=dst, in_=src)
+            else:
+                nc.vector.tensor_copy(out=dst, in_=src)
+            state[("wg", i)] = wg
+
+        def quant_w(i):
+            ww = cpool.tile([P, ND], U32, name="ww", tag="ww", align_bytes=64)
+            ws = cpool.tile([P, ND], U8, name="ws", tag="ws", align_bytes=64)
+            wg = state[("wg", i)]
+            nc.vector.quantize_mx(out=ww[:].bitcast(FP8X4), scales=ws[:], in_=wg[:].rearrange("p d t -> p (d t)"))
+            state[("codes", i)] = (ww, ws)
+
+        def stage1_mm(e):
+            eg, el = divmod(e, 4)
+            ps1 = psum.tile([P, 4, P], F32, name="ps1", tag="ps1")
+            for dc in range(4):
+                for g in range(2):
+                    ww, ws = state[("codes", 2 * e + g)]
+                    a = 4 * g + el
+                    nc.tensor.matmul_mx(
+                        out=ps1[:, dc, :],
+                        lhsT=ww[:, dc * P:(dc + 1) * P].bitcast(FP8X4),
+                        lhsT_scale=ws[:, dc * P:(dc + 1) * P],
+                        rhs=h_words[eg][:, a * P:(a + 1) * P].bitcast(FP8X4),
+                        rhs_scale=h_scales[eg][:, a * P:(a + 1) * P],
+                        start=(g == 0),
+                        stop=(g == 1),
+                    )
+            state[("ps1", e)] = ps1
+
+        def stage1_out(e):
+            ps1 = state[("ps1", e)]
+            for dc in range(4):
+                nc.scalar.activation(
+                    out=eoT[:, dc, :, NS * e:NS * (e + 1)],
+                    in_=ps1[:, dc, :].rearrange("p (b s) -> p b s", b=NB),
+                    func=ACT.Identity,
+                    bias=b2T[:, dc, e:e + 1],
+                    scale=1.0,
+                )
+
+        def sm_max(b):
+            x = lraw[b]
+            m1 = smpool.tile([P, 4, 256], BF16, name="m1", tag="m1")
+            nc.vector.tensor_tensor(out=m1[:], in0=x[:, :, 0:256], in1=x[:, :, 256:512], op=ALU.max)
+            m2 = smpool.tile([P, 4, 128], BF16, name="m2", tag="m2")
+            nc.vector.tensor_tensor(out=m2[:], in0=m1[:, :, 0:128], in1=m1[:, :, 128:256], op=ALU.max)
+            mx = smpool.tile([P, 4], F32, name="mx", tag="mx")
+            nc.vector.tensor_reduce(out=mx[:], in_=m2[:], axis=AXIS.X, op=ALU.max)
+            nmax = smpool.tile([P, 4], F32, name="nmax", tag="nmax")
+            nc.vector.tensor_scalar(out=nmax[:], in0=mx[:], scalar1=-1.0, scalar2=None, op0=ALU.mult)
+            state[("nmax", b)] = nmax
+            state[("ssum", b)] = [smpool.tile([P, 1], F32, name="ssum%d" % j, tag="ssum%d" % j) for j in range(4)]
+            state[("rinv", b)] = [smpool.tile([P, 1], F32, name="rinv%d" % j, tag="rinv%d" % j) for j in range(4)]
+            state[("gc", b)] = smpool.tile([P, 4, P, 4], BF16, name="gc", tag="gc", align_bytes=64)
+
+        def sm_exp(b, j):
+            ef = epool.tile([P, 512], F32, name="ef", tag="ef")
+            nc.scalar.activation(
+                out=ef[:], in_=lraw[b][:, j, :], func=ACT.Exp,
+                bias=state[("nmax", b)][:, j:j + 1], scale=1.0, accum_out=state[("ssum", b)][j][:],
+            )
+            state[("ef", b, j)] = ef
+
+        def sm_scale(b, j):
+            rinv = state[("rinv", b)][j]
+            nc.vector.reciprocal(out=rinv[:], in_=state[("ssum", b)][j][:])
+            cw = epool.tile([P, 512], BF16, name="cw", tag="cw")
+            nc.vector.tensor_scalar(out=cw[:], in0=state[("ef", b, j)][:], scalar1=rinv[:], scalar2=None, op0=ALU.mult)
+            if j % 2 == 0:
+                state[("cps", b, j // 2)] = psum.tile([P, 2, 4, P], BF16, name="cps", tag="cps")
+            cps = state[("cps", b, j // 2)]
+            for t in range(4):
+                nc.tensor.transpose(cps[:, j % 2, t, :], cw[:, t * P:(t + 1) * P], ident_b[:])
+
+        def sm_out(b, jp):
+            gc = state[("gc", b)]
+            nc.scalar.copy(out=gc[:, 2 * jp:2 * jp + 2, :, :], in_=state[("cps", b, jp)][:].rearrange("p j t l -> p j l t"))
+
+        def sm_quant(b):
+            nc.vector.quantize_mx(
+                out=cw_words[b][:].bitcast(FP8X4), scales=cw_scales[b][:],
+                in_=state[("gc", b)][:].rearrange("p j l t -> p (j l t)"),
+            )
+
+        def eo_tr(b, dh):
+            tps = psum.tile([P, 4, 256], BF16, name="tps", tag=TPS_TAGS[2 * b + dh])
+            for t in range(4):
+                for dl in range(2):
+                    nc.tensor.transpose(
+                        tps[:, t, dl * P:(dl + 1) * P],
+                        eoT[:, 2 * dh + dl, b, t * P:(t + 1) * P],
+                        ident_b[:],
+                    )
+            state[("tps", b, dh)] = tps
+
+        def eo_out(b, dh):
+            dst = eo_grouped[b][:, 256 * dh:256 * (dh + 1), :]
+            src = state[("tps", b, dh)][:].rearrange("p t d -> p d t")
+            if dh == 0:
+                nc.scalar.copy(out=dst, in_=src)
+            else:
+                nc.vector.tensor_copy(out=dst, in_=src)
+
+        def eo_quant(b):
+            nc.vector.quantize_mx(
+                out=eo_words[b][:].bitcast(FP8X4), scales=eo_scales[b][:],
+                in_=eo_grouped[b][:].rearrange("p d t -> p (d t)"),
+            )
+
+        def combine_mm(b, j):
+            ps2 = psum.tile([P, ND], F32, name="ps2", tag=("ps2", "ps1")[j % 2])
+            nc.tensor.matmul_mx(
+                out=ps2[:],
+                lhsT=cw_words[b][:, j * P:(j + 1) * P].bitcast(FP8X4),
+                lhsT_scale=cw_scales[b][:, j * P:(j + 1) * P],
+                rhs=eo_words[b][:].bitcast(FP8X4),
+                rhs_scale=eo_scales[b][:],
+                start=True,
+                stop=True,
+            )
+            state[("ps2", b, j)] = ps2
+
+        def combine_out(b, j):
+            if j == 0:
+                state[("ob", b)] = opool.tile([P, 4, ND], F32, name="ob", tag="ob")
+            ob = state[("ob", b)]
+            if j % 2 == 0:
+                nc.scalar.copy(out=ob[:, j, :], in_=state[("ps2", b, j)][:])
+            else:
+                nc.vector.tensor_copy(out=ob[:, j, :], in_=state[("ps2", b, j)][:])
+                dram = out[b].rearrange("(p j) d -> p j d", j=4)
+                nc.sync.dma_start(out=dram[:, j - 1:j + 1, :], in_=ob[:, j - 1:j + 1, :])
+
+        def combine(b):
+            for j in range(4):
+                combine_mm(b, j)
+                combine_out(b, j)
+
+        def bias_tr():
+            bps = psum.tile([P, 4, P], BF16, name="bps", tag="ps2")
+            for dc in range(4):
+                nc.tensor.transpose(bps[:, dc, :], b2z[:, dc * P:(dc + 1) * P], ident_b[:])
+            state["bps"] = bps
+
+        def bias_out():
+            nc.vector.tensor_copy(out=b2T[:], in_=state["bps"][:, :, 0:NE])
+
+        extras = {}
+
+        def at(slot, fn, *args):
+            extras[slot] = extras.get(slot, []) + [(fn, args)]
+
+        def plan_softmax(b, s0, exp_slots, scale_slots, out_slots, quant_slot):
+            at(s0, sm_max, b)
+            for j in range(4):
+                at(exp_slots[j], sm_exp, b, j)
+                at(scale_slots[j], sm_scale, b, j)
+            for jp in range(2):
+                at(out_slots[jp], sm_out, b, jp)
+            at(quant_slot, sm_quant, b)
+
+        plan_softmax(0, -2, (-2, -2, -2, -2), (1, 1, 2, 2), (2, 3), 6)
+        plan_softmax(1, 1, (1, 1, 2, 2), (3, 3, 4, 4), (5, 6), 9)
+        plan_softmax(2, 11, (12, 13, 14, 15), (14, 15, 16, 17), (17, 19), 23)
+        plan_softmax(3, 23, (24, 25, 30, 31), (26, 27, 34, 34), (29, 36), 37)
+        at(-2, bias_tr)
+        for b in range(NB):
+            at(-1, h_tile, 0, b)
+        at(3, bias_out)
+        at(2, h_quant, 0)
+        for eg in range(1, 4):
+            for b in range(NB):
+                at(8 * eg - 4 + b, h_tile, eg, b)
+            at(8 * eg + 1, h_quant, eg)
+        at(0, load_h, 1)
+        at(2, load_logits, 2)
+        at(4, load_logits, 3)
+        at(8, load_h, 2)
+        at(16, load_h, 3)
+
+        with ExitStack() as early:
+            hpool = early.enter_context(tc.tile_pool(name="hpool", bufs=4))
+            ghpool = early.enter_context(tc.tile_pool(name="ghpool", bufs=1))
+            wpool = early.enter_context(tc.tile_pool(name="wpool", bufs=W_BUFS))
+            gpool = early.enter_context(tc.tile_pool(name="gpool", bufs=6))
+            cpool = early.enter_context(tc.tile_pool(name="cpool", bufs=6))
+
+            nc.vector.memset(b2z[:], 0.0)
+            load_logits(0)
+            nc.sync.dma_start(out=b2z[0:NE, :], in_=b2)
+            load_w(0)
+            load_logits(1)
+            load_h(0)
+            for e in range(1, W_BUFS - 1):
+                load_w(e)
+
+            for s in range(-2, LAST_SLOT + 1):
+                if 0 <= s < N_UNITS and s % 2 == 0 and s // 2 + W_BUFS - 1 < NE:
+                    load_w(s // 2 + W_BUFS - 1)
+                if s + S_AHEAD in S_UNITS:
+                    regroup_w(s + S_AHEAD)
+                if 0 <= s < N_UNITS and s not in S_UNITS:
+                    regroup_w(s)
+                if 0 <= s - Q_LAG < N_UNITS:
+                    quant_w(s - Q_LAG)
+                    if (s - Q_LAG) % 2 == 1:
+                        stage1_mm((s - Q_LAG) // 2)
+                for fn, args in extras.get(s, []):
+                    fn(*args)
+                if 0 <= s - Q_LAG - 1 < N_UNITS and (s - Q_LAG - 1) % 2 == 1:
+                    stage1_out((s - Q_LAG - 1) // 2)
+
+        with ExitStack() as late:
+            tpool = late.enter_context(tc.tile_pool(name="tpool", bufs=1))
+            opool = late.enter_context(tc.tile_pool(name="opool", bufs=4))
+            eo_grouped = [tpool.tile([P, ND, 4], BF16, name="eo_grouped%d" % b, align_bytes=64) for b in range(NB)]
+            eo_words = [tpool.tile([P, ND], U32, name="eo_words%d" % b, align_bytes=64) for b in range(NB)]
+            eo_scales = [tpool.tile([P, ND], U8, name="eo_scales%d" % b, align_bytes=64) for b in range(NB)]
+            for fn, args in extras.get(LAST_SLOT + 1, []):
+                fn(*args)
+            for b in range(3):
+                eo_tr(b, 0)
+                eo_tr(b, 1)
+            eo_out(0, 0)
+            eo_out(0, 1)
+            eo_out(1, 0)
+            eo_out(1, 1)
+            eo_quant(0)
+            eo_tr(3, 0)
+            eo_tr(3, 1)
+            for fn, args in extras.get(LAST_SLOT + 2, []):
+                fn(*args)
+            combine(0)
+            eo_quant(1)
+            eo_out(2, 0)
+            eo_out(2, 1)
+            combine(1)
+            eo_quant(2)
+            eo_out(3, 0)
+            eo_out(3, 1)
+            combine(2)
+            eo_quant(3)
+            combine(3)

@@ -17,12 +17,11 @@ NB, NL, ND, NE, NS, NH = 4, 512, 512, 16, 32, 1024
 FLOPS = 2 * NB * NE * NS * NH * ND + 2 * NB * NL * NE * NS * ND
 
 W_BUFS = 5
-N_UNITS = 2 * NE
-S_UNITS = (6, 9, 12, 15, 18, 21, 24, 27, 30)
+S_HALVES = ((1, 1), (3, 1), (5, 1), (7, 1), (9, 1), (11, 1), (13, 1))
 S_AHEAD = 3
-Q_LAG = 2
-LAST_SLOT = N_UNITS + Q_LAG + 1
-TPS_TAGS = ("tr", "tr", "ps1", "ps1", "cps", "cps", "tr", "tr")
+LAST_SLOT = 34
+SPLIT = (14, 15)
+TPS_TAGS = ("tr", "ps1", "tr", "ps1", "tr", "ps1", "tr", "ps1")
 
 
 def tile_softmoe_pb_kernel(tc, h, w2, b2, logits, out):
@@ -30,9 +29,8 @@ def tile_softmoe_pb_kernel(tc, h, w2, b2, logits, out):
     with ExitStack() as ctx:
         const = ctx.enter_context(tc.tile_pool(name="const", bufs=1))
         smpool = ctx.enter_context(tc.tile_pool(name="smpool", bufs=2))
-        epool = ctx.enter_context(tc.tile_pool(name="epool", bufs=4))
+        epool = ctx.enter_context(tc.tile_pool(name="epool", bufs=6))
         psum = ctx.enter_context(tc.psum_pool(name="psum", bufs=2))
-        ctx.enter_context(tc.manual_schedule())
 
         ident_f = const.tile([P, P], F32, name="ident_f")
         make_identity(nc, ident_f[:])
@@ -56,11 +54,7 @@ def tile_softmoe_pb_kernel(tc, h, w2, b2, logits, out):
             wraw = wpool.tile([P, 8, ND], BF16, name="wraw", tag="wraw")
             src = w2[e].rearrange("(c p r) d -> p c (r d)", c=4, p=P, r=2)
             dst = wraw[:].rearrange("p (c r) d -> p c (r d)", c=4, r=2)
-            if e == 0:
-                nc.sync.dma_start(out=dst[:, 0:2, :], in_=src[:, 0:2, :])
-                nc.sync.dma_start(out=dst[:, 2:4, :], in_=src[:, 2:4, :])
-            else:
-                nc.sync.dma_start(out=dst, in_=src)
+            nc.sync.dma_start(out=dst, in_=src)
             wtiles[e] = wraw
 
         def load_h(eg):
@@ -92,35 +86,52 @@ def tile_softmoe_pb_kernel(tc, h, w2, b2, logits, out):
         def h_quant(eg):
             nc.vector.quantize_mx(out=h_words[eg][:].bitcast(FP8X4), scales=h_scales[eg][:], in_=state[("gh", eg)][:])
 
-        def regroup_w(i):
-            e, g = divmod(i, 2)
-            wg = gpool.tile([P, ND, 4], BF16, name="wg", tag="wg", align_bytes=64)
-            dst = wg[:].rearrange("p (c i) t -> p c t i", i=4)
+        def grouped_tile(e):
+            if ("wg", e) not in state:
+                state[("wg", e)] = gpool.tile([P, 2, ND, 4], BF16, name="wg", tag="wg", align_bytes=64)
+            return state[("wg", e)]
+
+        def regroup_half(e, g, on_scalar):
+            wg = grouped_tile(e)
+            dst = wg[:, g, :, :].rearrange("p (c i) t -> p c t i", i=4)
             src = wtiles[e][:, 4 * g:4 * g + 4, :].rearrange("p t (c i) -> p c t i", i=4)
-            if i in S_UNITS:
+            if on_scalar:
                 nc.scalar.copy(out=dst, in_=src)
             else:
                 nc.vector.tensor_copy(out=dst, in_=src)
-            state[("wg", i)] = wg
 
-        def quant_w(i):
-            ww = cpool.tile([P, ND], U32, name="ww", tag="ww", align_bytes=64)
-            ws = cpool.tile([P, ND], U8, name="ws", tag="ws", align_bytes=64)
-            wg = state[("wg", i)]
-            nc.vector.quantize_mx(out=ww[:].bitcast(FP8X4), scales=ws[:], in_=wg[:].rearrange("p d t -> p (d t)"))
-            state[("codes", i)] = (ww, ws)
+        def regroup_vector(e):
+            halves = [g for g in range(2) if (e, g) not in S_HALVES]
+            if len(halves) == 2:
+                wg = grouped_tile(e)
+                nc.vector.tensor_copy(
+                    out=wg[:].rearrange("p g (c i) t -> p g c t i", i=4),
+                    in_=wtiles[e][:].rearrange("p (g t) (c i) -> p g c t i", g=2, i=4),
+                )
+            else:
+                for g in halves:
+                    regroup_half(e, g, False)
+
+        def quant_w(e):
+            ww = cpool.tile([P, 2 * ND], U32, name="ww", tag="ww", align_bytes=64)
+            ws = cpool.tile([P, 2 * ND], U8, name="ws", tag="ws", align_bytes=64)
+            nc.vector.quantize_mx(
+                out=ww[:].bitcast(FP8X4), scales=ws[:], in_=state[("wg", e)][:].rearrange("p g d t -> p (g d t)")
+            )
+            state[("codes", e)] = (ww, ws)
 
         def stage1_mm(e):
             eg, el = divmod(e, 4)
             ps1 = psum.tile([P, 4, P], F32, name="ps1", tag="ps1")
+            ww, ws = state[("codes", e)]
             for dc in range(4):
                 for g in range(2):
-                    ww, ws = state[("codes", 2 * e + g)]
                     a = 4 * g + el
+                    c0 = g * ND + dc * P
                     nc.tensor.matmul_mx(
                         out=ps1[:, dc, :],
-                        lhsT=ww[:, dc * P:(dc + 1) * P].bitcast(FP8X4),
-                        lhsT_scale=ws[:, dc * P:(dc + 1) * P],
+                        lhsT=ww[:, c0:c0 + P].bitcast(FP8X4),
+                        lhsT_scale=ws[:, c0:c0 + P],
                         rhs=h_words[eg][:, a * P:(a + 1) * P].bitcast(FP8X4),
                         rhs_scale=h_scales[eg][:, a * P:(a + 1) * P],
                         start=(g == 0),
@@ -139,43 +150,87 @@ def tile_softmoe_pb_kernel(tc, h, w2, b2, logits, out):
                     scale=1.0,
                 )
 
+        def split_unit(e, dh):
+            eg, el = divmod(e, 4)
+            wg = gpool.tile([P, 2, 256, 4], BF16, name="wgs", tag="wgs", align_bytes=64, bufs=2)
+            nc.vector.tensor_copy(
+                out=wg[:].rearrange("p g (c i) t -> p g c t i", i=4),
+                in_=wtiles[e][:, :, 256 * dh:256 * (dh + 1)].rearrange("p (g t) (c i) -> p g c t i", g=2, i=4),
+            )
+            state[("wgs", e, dh)] = wg
+
+        def split_quant(e, dh):
+            eg, el = divmod(e, 4)
+            ww = cpool.tile([P, ND], U32, name="wws", tag="wws", align_bytes=64, bufs=2)
+            ws = cpool.tile([P, ND], U8, name="wss", tag="wss", align_bytes=64, bufs=2)
+            nc.vector.quantize_mx(
+                out=ww[:].bitcast(FP8X4), scales=ws[:], in_=state[("wgs", e, dh)][:].rearrange("p g d t -> p (g d t)")
+            )
+            ps1 = psum.tile([P, 2, P], F32, name="ps1", tag="ps1")
+            for dl in range(2):
+                for g in range(2):
+                    a = 4 * g + el
+                    c0 = g * 256 + dl * P
+                    nc.tensor.matmul_mx(
+                        out=ps1[:, dl, :],
+                        lhsT=ww[:, c0:c0 + P].bitcast(FP8X4),
+                        lhsT_scale=ws[:, c0:c0 + P],
+                        rhs=h_words[eg][:, a * P:(a + 1) * P].bitcast(FP8X4),
+                        rhs_scale=h_scales[eg][:, a * P:(a + 1) * P],
+                        start=(g == 0),
+                        stop=(g == 1),
+                    )
+            for dl in range(2):
+                nc.scalar.activation(
+                    out=eoT[:, 2 * dh + dl, :, NS * e:NS * (e + 1)],
+                    in_=ps1[:, dl, :].rearrange("p (b s) -> p b s", b=NB),
+                    func=ACT.Identity,
+                    bias=b2T[:, 2 * dh + dl, e:e + 1],
+                    scale=1.0,
+                )
+
         def sm_max(b):
             x = lraw[b]
-            m1 = smpool.tile([P, 4, 256], BF16, name="m1", tag="m1")
+            m1 = smpool.tile([P, 4, 256], BF16, name="m1", tag="m1", bufs=1)
             nc.vector.tensor_tensor(out=m1[:], in0=x[:, :, 0:256], in1=x[:, :, 256:512], op=ALU.max)
-            m2 = smpool.tile([P, 4, 128], BF16, name="m2", tag="m2")
+            m2 = smpool.tile([P, 4, 128], BF16, name="m2", tag="m2", bufs=1)
             nc.vector.tensor_tensor(out=m2[:], in0=m1[:, :, 0:128], in1=m1[:, :, 128:256], op=ALU.max)
             mx = smpool.tile([P, 4], F32, name="mx", tag="mx")
             nc.vector.tensor_reduce(out=mx[:], in_=m2[:], axis=AXIS.X, op=ALU.max)
             nmax = smpool.tile([P, 4], F32, name="nmax", tag="nmax")
             nc.vector.tensor_scalar(out=nmax[:], in0=mx[:], scalar1=-1.0, scalar2=None, op0=ALU.mult)
             state[("nmax", b)] = nmax
-            state[("ssum", b)] = [smpool.tile([P, 1], F32, name="ssum%d" % j, tag="ssum%d" % j) for j in range(4)]
-            state[("rinv", b)] = [smpool.tile([P, 1], F32, name="rinv%d" % j, tag="rinv%d" % j) for j in range(4)]
+            state[("ssum", b)] = smpool.tile([P, 4], F32, name="ssum", tag="ssum")
             state[("gc", b)] = smpool.tile([P, 4, P, 4], BF16, name="gc", tag="gc", align_bytes=64)
 
         def sm_exp(b, j):
             ef = epool.tile([P, 512], F32, name="ef", tag="ef")
             nc.scalar.activation(
                 out=ef[:], in_=lraw[b][:, j, :], func=ACT.Exp,
-                bias=state[("nmax", b)][:, j:j + 1], scale=1.0, accum_out=state[("ssum", b)][j][:],
+                bias=state[("nmax", b)][:, j:j + 1], scale=1.0, accum_out=state[("ssum", b)][:, j:j + 1],
             )
             state[("ef", b, j)] = ef
 
-        def sm_scale(b, j):
-            rinv = state[("rinv", b)][j]
-            nc.vector.reciprocal(out=rinv[:], in_=state[("ssum", b)][j][:])
-            cw = epool.tile([P, 512], BF16, name="cw", tag="cw")
-            nc.vector.tensor_scalar(out=cw[:], in0=state[("ef", b, j)][:], scalar1=rinv[:], scalar2=None, op0=ALU.mult)
-            if j % 2 == 0:
-                state[("cps", b, j // 2)] = psum.tile([P, 2, 4, P], BF16, name="cps", tag="cps")
-            cps = state[("cps", b, j // 2)]
-            for t in range(4):
-                nc.tensor.transpose(cps[:, j % 2, t, :], cw[:, t * P:(t + 1) * P], ident_b[:])
+        def sm_norm(b):
+            rinv = smpool.tile([P, 4], F32, name="rinv", tag="rinv")
+            nc.vector.reciprocal(out=rinv[:], in_=state[("ssum", b)][:])
+            dg = smpool.tile([P, 4, P], F32, name="dg", tag="dg")
+            for j in range(4):
+                nc.vector.tensor_scalar(out=dg[:, j, :], in0=ident_f[:], scalar1=rinv[:, j:j + 1], scalar2=None, op0=ALU.mult)
+            state[("dg", b)] = dg
 
-        def sm_out(b, jp):
+        def sm_tr(b, j):
+            cps = psum.tile([P, 4, P], F32, name="cps", tag="cps")
+            ef = state[("ef", b, j)]
+            for t in range(4):
+                nc.tensor.matmul(
+                    out=cps[:, t, :], lhsT=ef[:, t * P:(t + 1) * P], rhs=state[("dg", b)][:, j, :], start=True, stop=True
+                )
+            state[("cps", b, j)] = cps
+
+        def sm_out(b, j):
             gc = state[("gc", b)]
-            nc.scalar.copy(out=gc[:, 2 * jp:2 * jp + 2, :, :], in_=state[("cps", b, jp)][:].rearrange("p j t l -> p j l t"))
+            nc.scalar.copy(out=gc[:, j, :, :], in_=state[("cps", b, j)][:].rearrange("p t l -> p l t"))
 
         def sm_quant(b):
             nc.vector.quantize_mx(
@@ -197,7 +252,7 @@ def tile_softmoe_pb_kernel(tc, h, w2, b2, logits, out):
         def eo_out(b, dh):
             dst = eo_grouped[b][:, 256 * dh:256 * (dh + 1), :]
             src = state[("tps", b, dh)][:].rearrange("p t d -> p d t")
-            if dh == 0:
+            if (b + dh) % 2 == 0:
                 nc.scalar.copy(out=dst, in_=src)
             else:
                 nc.vector.tensor_copy(out=dst, in_=src)
@@ -209,7 +264,7 @@ def tile_softmoe_pb_kernel(tc, h, w2, b2, logits, out):
             )
 
         def combine_mm(b, j):
-            ps2 = psum.tile([P, ND], F32, name="ps2", tag=("ps2", "ps1")[j % 2])
+            ps2 = psum.tile([P, ND], F32, name="ps2", tag=("ps2", "cps")[j % 2])
             nc.tensor.matmul_mx(
                 out=ps2[:],
                 lhsT=cw_words[b][:, j * P:(j + 1) * P].bitcast(FP8X4),
@@ -251,19 +306,32 @@ def tile_softmoe_pb_kernel(tc, h, w2, b2, logits, out):
         def at(slot, fn, *args):
             extras[slot] = extras.get(slot, []) + [(fn, args)]
 
-        def plan_softmax(b, s0, exp_slots, scale_slots, out_slots, quant_slot):
-            at(s0, sm_max, b)
+        def plan_softmax(b, s_max, s_exp, s_norm, s_q):
+            at(s_max, sm_max, b)
             for j in range(4):
-                at(exp_slots[j], sm_exp, b, j)
-                at(scale_slots[j], sm_scale, b, j)
-            for jp in range(2):
-                at(out_slots[jp], sm_out, b, jp)
-            at(quant_slot, sm_quant, b)
+                at(s_exp[j], sm_exp, b, j)
+            at(s_norm, sm_norm, b)
+            for j in range(4):
+                at(s_norm + j, sm_tr, b, j)
+                at(s_norm + j + 1, sm_out, b, j)
+            at(s_q, sm_quant, b)
 
-        plan_softmax(0, -2, (-2, -2, -2, -2), (1, 1, 2, 2), (2, 3), 6)
-        plan_softmax(1, 1, (1, 1, 2, 2), (3, 3, 4, 4), (5, 6), 9)
-        plan_softmax(2, 11, (12, 13, 14, 15), (14, 15, 16, 17), (17, 19), 23)
-        plan_softmax(3, 23, (24, 25, 30, 31), (26, 27, 34, 34), (29, 36), 37)
+        def softmax_all(b):
+            sm_max(b)
+            for j in range(4):
+                sm_exp(b, j)
+            sm_norm(b)
+            for j in range(4):
+                sm_tr(b, j)
+                sm_out(b, j)
+            sm_quant(b)
+
+        plan_softmax(0, -2, (-2, -2, -2, -2), 1, 7)
+        plan_softmax(1, 1, (1, 1, 2, 2), 5, 11)
+        plan_softmax(2, 12, (13, 14, 15, 16), 18, 24)
+        at(20, sm_max, 3)
+        for j in range(4):
+            at(21 + j, sm_exp, 3, j)
         at(-2, bias_tr)
         for b in range(NB):
             at(-1, h_tile, 0, b)
@@ -274,8 +342,7 @@ def tile_softmoe_pb_kernel(tc, h, w2, b2, logits, out):
                 at(8 * eg - 4 + b, h_tile, eg, b)
             at(8 * eg + 1, h_quant, eg)
         at(0, load_h, 1)
-        at(2, load_logits, 2)
-        at(4, load_logits, 3)
+        at(2, load_logits, 3)
         at(8, load_h, 2)
         at(16, load_h, 3)
 
@@ -283,33 +350,45 @@ def tile_softmoe_pb_kernel(tc, h, w2, b2, logits, out):
             hpool = early.enter_context(tc.tile_pool(name="hpool", bufs=4))
             ghpool = early.enter_context(tc.tile_pool(name="ghpool", bufs=1))
             wpool = early.enter_context(tc.tile_pool(name="wpool", bufs=W_BUFS))
-            gpool = early.enter_context(tc.tile_pool(name="gpool", bufs=6))
-            cpool = early.enter_context(tc.tile_pool(name="cpool", bufs=6))
+            gpool = early.enter_context(tc.tile_pool(name="gpool", bufs=3))
+            cpool = early.enter_context(tc.tile_pool(name="cpool", bufs=3))
 
             nc.vector.memset(b2z[:], 0.0)
             load_logits(0)
             nc.sync.dma_start(out=b2z[0:NE, :], in_=b2)
             load_w(0)
             load_logits(1)
+            load_w(1)
             load_h(0)
-            for e in range(1, W_BUFS - 1):
-                load_w(e)
+            load_w(2)
+            load_w(3)
+            load_logits(2)
 
             for s in range(-2, LAST_SLOT + 1):
-                if 0 <= s < N_UNITS and s % 2 == 0 and s // 2 + W_BUFS - 1 < NE:
-                    load_w(s // 2 + W_BUFS - 1)
-                if s + S_AHEAD in S_UNITS:
-                    regroup_w(s + S_AHEAD)
-                if 0 <= s < N_UNITS and s not in S_UNITS:
-                    regroup_w(s)
-                if 0 <= s - Q_LAG < N_UNITS:
-                    quant_w(s - Q_LAG)
-                    if (s - Q_LAG) % 2 == 1:
-                        stage1_mm((s - Q_LAG) // 2)
+                e = s // 2
+                if 0 <= s < 2 * NE and s % 2 == 0 and e + W_BUFS - 1 < NE:
+                    load_w(e + W_BUFS - 1)
+                for (se, sg) in S_HALVES:
+                    if 2 * se - S_AHEAD == s:
+                        regroup_half(se, sg, True)
+                if 0 <= s < 2 * NE and s % 2 == 0 and e not in SPLIT:
+                    regroup_vector(e)
+                qe = (s - 3) // 2 if s % 2 == 1 else -1
+                if 0 <= qe < NE and qe not in SPLIT:
+                    quant_w(qe)
+                    stage1_mm(qe)
                 for fn, args in extras.get(s, []):
                     fn(*args)
-                if 0 <= s - Q_LAG - 1 < N_UNITS and (s - Q_LAG - 1) % 2 == 1:
-                    stage1_out((s - Q_LAG - 1) // 2)
+                oe = (s - 4) // 2 if s % 2 == 0 else -1
+                if 0 <= oe < NE and oe not in SPLIT:
+                    stage1_out(oe)
+                if s == 2 * SPLIT[0]:
+                    units = [(se, dh) for dh in range(2) for se in SPLIT]
+                    for k in range(len(units) + 1):
+                        if k < len(units):
+                            split_unit(*units[k])
+                        if k >= 1:
+                            split_quant(*units[k - 1])
 
         with ExitStack() as late:
             tpool = late.enter_context(tc.tile_pool(name="tpool", bufs=1))
@@ -317,28 +396,16 @@ def tile_softmoe_pb_kernel(tc, h, w2, b2, logits, out):
             eo_grouped = [tpool.tile([P, ND, 4], BF16, name="eo_grouped%d" % b, align_bytes=64) for b in range(NB)]
             eo_words = [tpool.tile([P, ND], U32, name="eo_words%d" % b, align_bytes=64) for b in range(NB)]
             eo_scales = [tpool.tile([P, ND], U8, name="eo_scales%d" % b, align_bytes=64) for b in range(NB)]
-            for fn, args in extras.get(LAST_SLOT + 1, []):
-                fn(*args)
-            for b in range(3):
+            for b in range(NB):
                 eo_tr(b, 0)
+                eo_out(b, 0)
+            sm_norm(3)
+            for j in range(4):
+                sm_tr(3, j)
+                sm_out(3, j)
+            sm_quant(3)
+            for b in range(NB):
                 eo_tr(b, 1)
-            eo_out(0, 0)
-            eo_out(0, 1)
-            eo_out(1, 0)
-            eo_out(1, 1)
-            eo_quant(0)
-            eo_tr(3, 0)
-            eo_tr(3, 1)
-            for fn, args in extras.get(LAST_SLOT + 2, []):
-                fn(*args)
-            combine(0)
-            eo_quant(1)
-            eo_out(2, 0)
-            eo_out(2, 1)
-            combine(1)
-            eo_quant(2)
-            eo_out(3, 0)
-            eo_out(3, 1)
-            combine(2)
-            eo_quant(3)
-            combine(3)
+                eo_out(b, 1)
+                eo_quant(b)
+                combine(b)

@@ -17,7 +17,7 @@ NB, NL, ND, NE, NS, NH = 4, 512, 512, 16, 32, 1024
 FLOPS = 2 * NB * NE * NS * NH * ND + 2 * NB * NL * NE * NS * ND
 
 W_BUFS = 5
-S_HALVES = ((1, 1), (3, 1), (5, 1), (7, 1), (9, 1), (11, 1), (13, 1))
+S_HALVES = ((1, 1), (2, 1), (3, 1), (5, 1), (6, 1), (7, 1), (9, 1), (10, 1), (11, 1), (13, 1))
 S_AHEAD = 3
 LAST_SLOT = 34
 SPLIT = (14, 15)

@@ -17,10 +17,10 @@ NB, NL, ND, NE, NS, NH = 4, 512, 512, 16, 32, 1024
 FLOPS = 2 * NB * NE * NS * NH * ND + 2 * NB * NL * NE * NS * ND
 
 W_BUFS = 5
-S_HALVES = ((1, 1), (2, 1), (3, 1), (5, 1), (6, 1), (7, 1), (9, 1), (10, 1), (11, 1), (13, 1))
+S_HALVES = ((1, 1), (3, 1), (5, 1), (7, 1), (9, 1))
 S_AHEAD = 3
-LAST_SLOT = 34
-SPLIT = (14, 15)
+LAST_SLOT = 2 * 12 + 3
+SPLIT = (12, 13, 14, 15)
 TPS_TAGS = ("tr", "ps1", "tr", "ps1", "tr", "ps1", "tr", "ps1")
 
 
@@ -29,7 +29,7 @@ def tile_softmoe_pb_kernel(tc, h, w2, b2, logits, out):
     with ExitStack() as ctx:
         const = ctx.enter_context(tc.tile_pool(name="const", bufs=1))
         smpool = ctx.enter_context(tc.tile_pool(name="smpool", bufs=2))
-        epool = ctx.enter_context(tc.tile_pool(name="epool", bufs=6))
+        epool = ctx.enter_context(tc.tile_pool(name="epool", bufs=5))
         psum = ctx.enter_context(tc.psum_pool(name="psum", bufs=2))
 
         ident_f = const.tile([P, P], F32, name="ident_f")
@@ -41,7 +41,8 @@ def tile_softmoe_pb_kernel(tc, h, w2, b2, logits, out):
         h_scales = [const.tile([P, 1024], U8, name="h_scales%d" % eg, align_bytes=64) for eg in range(4)]
         cw_words = [const.tile([P, NL], U32, name="cw_words%d" % b, align_bytes=64) for b in range(NB)]
         cw_scales = [const.tile([P, NL], U8, name="cw_scales%d" % b, align_bytes=64) for b in range(NB)]
-        lraw = [const.tile([P, 4, 512], BF16, name="lraw%d" % b) for b in range(NB)]
+        shared = ctx.enter_context(tc.tile_pool(name="shared", bufs=4))
+        lraw = [shared.tile([P, 4, 512], BF16, name="lraw%d" % b, tag="big", align_bytes=64) for b in range(NB)]
         eoT = const.tile([P, 4, NB, 512], BF16, name="eoT")
         b2z = const.tile([P, ND], BF16, name="b2z")
         b2T = const.tile([P, 4, NE], F32, name="b2T")
@@ -252,45 +253,38 @@ def tile_softmoe_pb_kernel(tc, h, w2, b2, logits, out):
         def eo_out(b, dh):
             dst = eo_grouped[b][:, 256 * dh:256 * (dh + 1), :]
             src = state[("tps", b, dh)][:].rearrange("p t d -> p d t")
-            if (b + dh) % 2 == 0:
+            if dh == 0 or b % 2 == 0:
                 nc.scalar.copy(out=dst, in_=src)
             else:
                 nc.vector.tensor_copy(out=dst, in_=src)
 
-        def eo_quant(b):
+        def eo_quant(b, dh):
             nc.vector.quantize_mx(
-                out=eo_words[b][:].bitcast(FP8X4), scales=eo_scales[b][:],
-                in_=eo_grouped[b][:].rearrange("p d t -> p (d t)"),
+                out=eo_words[b][:, 256 * dh:256 * (dh + 1)].bitcast(FP8X4), scales=eo_scales[b][:, 256 * dh:256 * (dh + 1)],
+                in_=eo_grouped[b][:, 256 * dh:256 * (dh + 1), :].rearrange("p d t -> p (d t)"),
             )
 
-        def combine_mm(b, j):
-            ps2 = psum.tile([P, ND], F32, name="ps2", tag=("ps2", "cps")[j % 2])
-            nc.tensor.matmul_mx(
-                out=ps2[:],
-                lhsT=cw_words[b][:, j * P:(j + 1) * P].bitcast(FP8X4),
-                lhsT_scale=cw_scales[b][:, j * P:(j + 1) * P],
-                rhs=eo_words[b][:].bitcast(FP8X4),
-                rhs_scale=eo_scales[b][:],
-                start=True,
-                stop=True,
-            )
-            state[("ps2", b, j)] = ps2
-
-        def combine_out(b, j):
-            if j == 0:
-                state[("ob", b)] = opool.tile([P, 4, ND], F32, name="ob", tag="ob")
-            ob = state[("ob", b)]
-            if j % 2 == 0:
-                nc.scalar.copy(out=ob[:, j, :], in_=state[("ps2", b, j)][:])
-            else:
-                nc.vector.tensor_copy(out=ob[:, j, :], in_=state[("ps2", b, j)][:])
-                dram = out[b].rearrange("(p j) d -> p j d", j=4)
-                nc.sync.dma_start(out=dram[:, j - 1:j + 1, :], in_=ob[:, j - 1:j + 1, :])
-
-        def combine(b):
-            for j in range(4):
-                combine_mm(b, j)
-                combine_out(b, j)
+        def combine(b, dh):
+            ob = opool.tile([P, 4, 256], F32, name="ob", tag="ob")
+            for jp in range(2):
+                ps2 = psum.tile([P, 2, 256], F32, name="ps2", tag=("ps2", "cps")[jp])
+                for jj in range(2):
+                    j = 2 * jp + jj
+                    nc.tensor.matmul_mx(
+                        out=ps2[:, jj, :],
+                        lhsT=cw_words[b][:, j * P:(j + 1) * P].bitcast(FP8X4),
+                        lhsT_scale=cw_scales[b][:, j * P:(j + 1) * P],
+                        rhs=eo_words[b][:, 256 * dh:256 * (dh + 1)].bitcast(FP8X4),
+                        rhs_scale=eo_scales[b][:, 256 * dh:256 * (dh + 1)],
+                        start=True,
+                        stop=True,
+                    )
+                if jp == 0 or (dh == 0 and b < 1):
+                    nc.scalar.copy(out=ob[:, 2 * jp:2 * jp + 2, :], in_=ps2[:])
+                else:
+                    nc.vector.tensor_copy(out=ob[:, 2 * jp:2 * jp + 2, :], in_=ps2[:])
+            dram = out[b].rearrange("(p j) d -> p j d", j=4)
+            nc.sync.dma_start(out=dram[:, :, 256 * dh:256 * (dh + 1)], in_=ob[:])
 
         def bias_tr():
             bps = psum.tile([P, 4, P], BF16, name="bps", tag="ps2")
@@ -329,9 +323,7 @@ def tile_softmoe_pb_kernel(tc, h, w2, b2, logits, out):
         plan_softmax(0, -2, (-2, -2, -2, -2), 1, 7)
         plan_softmax(1, 1, (1, 1, 2, 2), 5, 11)
         plan_softmax(2, 12, (13, 14, 15, 16), 18, 24)
-        at(20, sm_max, 3)
-        for j in range(4):
-            at(21 + j, sm_exp, 3, j)
+        plan_softmax(3, 17, (18, 19, 20, 21), 22, 27)
         at(-2, bias_tr)
         for b in range(NB):
             at(-1, h_tile, 0, b)
@@ -382,30 +374,20 @@ def tile_softmoe_pb_kernel(tc, h, w2, b2, logits, out):
                 oe = (s - 4) // 2 if s % 2 == 0 else -1
                 if 0 <= oe < NE and oe not in SPLIT:
                     stage1_out(oe)
-                if s == 2 * SPLIT[0]:
-                    units = [(se, dh) for dh in range(2) for se in SPLIT]
-                    for k in range(len(units) + 1):
-                        if k < len(units):
-                            split_unit(*units[k])
-                        if k >= 1:
-                            split_quant(*units[k - 1])
 
-        with ExitStack() as late:
-            tpool = late.enter_context(tc.tile_pool(name="tpool", bufs=1))
-            opool = late.enter_context(tc.tile_pool(name="opool", bufs=4))
-            eo_grouped = [tpool.tile([P, ND, 4], BF16, name="eo_grouped%d" % b, align_bytes=64) for b in range(NB)]
+            tpool = early.enter_context(tc.tile_pool(name="tpool", bufs=1))
+            opool = early.enter_context(tc.tile_pool(name="opool", bufs=3))
+            eo_grouped = [shared.tile([P, ND, 4], BF16, name="eo_grouped%d" % b, tag="big", align_bytes=64) for b in range(NB)]
             eo_words = [tpool.tile([P, ND], U32, name="eo_words%d" % b, align_bytes=64) for b in range(NB)]
             eo_scales = [tpool.tile([P, ND], U8, name="eo_scales%d" % b, align_bytes=64) for b in range(NB)]
-            for b in range(NB):
-                eo_tr(b, 0)
-                eo_out(b, 0)
-            sm_norm(3)
-            for j in range(4):
-                sm_tr(3, j)
-                sm_out(3, j)
-            sm_quant(3)
-            for b in range(NB):
-                eo_tr(b, 1)
-                eo_out(b, 1)
-                eo_quant(b)
-                combine(b)
+            for dh in range(2):
+                for k in range(len(SPLIT) + 1):
+                    if k < len(SPLIT):
+                        split_unit(SPLIT[k], dh)
+                    if k >= 1:
+                        split_quant(SPLIT[k - 1], dh)
+                for b in range(NB):
+                    eo_tr(b, dh)
+                    eo_out(b, dh)
+                    eo_quant(b, dh)
+                    combine(b, dh)

@@ -17,10 +17,11 @@ NB, NL, ND, NE, NS, NH = 4, 512, 512, 16, 32, 1024
 FLOPS = 2 * NB * NE * NS * NH * ND + 2 * NB * NL * NE * NS * ND
 
 W_BUFS = 5
-S_HALVES = ((1, 1), (3, 1), (5, 1), (7, 1), (9, 1))
+S_HALVES = ((1, 1), (5, 1), (9, 1))
 S_AHEAD = 3
 LAST_SLOT = 2 * 12 + 3
 SPLIT = (12, 13, 14, 15)
+SCALE_ON_VECTOR = ()
 TPS_TAGS = ("tr", "ps1", "tr", "ps1", "tr", "ps1", "tr", "ps1")
 
 
@@ -215,23 +216,27 @@ def tile_softmoe_pb_kernel(tc, h, w2, b2, logits, out):
         def sm_norm(b):
             rinv = smpool.tile([P, 4], F32, name="rinv", tag="rinv")
             nc.vector.reciprocal(out=rinv[:], in_=state[("ssum", b)][:])
-            dg = smpool.tile([P, 4, P], F32, name="dg", tag="dg")
-            for j in range(4):
-                nc.vector.tensor_scalar(out=dg[:, j, :], in0=ident_f[:], scalar1=rinv[:, j:j + 1], scalar2=None, op0=ALU.mult)
-            state[("dg", b)] = dg
+            state[("rinv", b)] = rinv
 
         def sm_tr(b, j):
-            cps = psum.tile([P, 4, P], F32, name="cps", tag="cps")
-            ef = state[("ef", b, j)]
+            cw = epool.tile([P, 512], BF16, name="cw", tag="cw", bufs=3)
+            rinv = state[("rinv", b)]
+            if j in SCALE_ON_VECTOR:
+                nc.vector.tensor_scalar(out=cw[:], in0=state[("ef", b, j)][:], scalar1=rinv[:, j:j + 1], scalar2=None, op0=ALU.mult)
+            else:
+                nc.scalar.activation(out=cw[:], in_=state[("ef", b, j)][:], func=ACT.Copy, scale=rinv[:, j:j + 1])
+            if j % 2 == 0:
+                state[("cps", b, j // 2)] = psum.tile([P, 2, 4, P], BF16, name="cps", tag="cps")
+            cps = state[("cps", b, j // 2)]
             for t in range(4):
-                nc.tensor.matmul(
-                    out=cps[:, t, :], lhsT=ef[:, t * P:(t + 1) * P], rhs=state[("dg", b)][:, j, :], start=True, stop=True
-                )
-            state[("cps", b, j)] = cps
+                nc.tensor.transpose(cps[:, j % 2, t, :], cw[:, t * P:(t + 1) * P], ident_b[:])
 
         def sm_out(b, j):
-            gc = state[("gc", b)]
-            nc.scalar.copy(out=gc[:, j, :, :], in_=state[("cps", b, j)][:].rearrange("p t l -> p l t"))
+            if j % 2 == 1:
+                gc = state[("gc", b)]
+                nc.scalar.copy(
+                    out=gc[:, j - 1:j + 1, :, :], in_=state[("cps", b, j // 2)][:].rearrange("p j t l -> p j l t")
+                )
 
         def sm_quant(b):
             nc.vector.quantize_mx(

@@ -95,8 +95,8 @@ def tile_softmoe_pb_kernel(tc, h, w2, b2, logits, out):
 
         def regroup_half(e, g, on_scalar):
             wg = grouped_tile(e)
-            dst = wg[:, g, :, :].rearrange("p (c i) t -> p c t i", i=4)
-            src = wtiles[e][:, 4 * g:4 * g + 4, :].rearrange("p t (c i) -> p c t i", i=4)
+            dst = wg[:, g, :, :].rearrange("p (c i) t -> p c t i", i=8)
+            src = wtiles[e][:, 4 * g:4 * g + 4, :].rearrange("p t (c i) -> p c t i", i=8)
             if on_scalar:
                 nc.scalar.copy(out=dst, in_=src)
             else:
@@ -107,8 +107,8 @@ def tile_softmoe_pb_kernel(tc, h, w2, b2, logits, out):
             if len(halves) == 2:
                 wg = grouped_tile(e)
                 nc.vector.tensor_copy(
-                    out=wg[:].rearrange("p g (c i) t -> p g c t i", i=4),
-                    in_=wtiles[e][:].rearrange("p (g t) (c i) -> p g c t i", g=2, i=4),
+                    out=wg[:].rearrange("p g (c i) t -> p g c t i", i=8),
+                    in_=wtiles[e][:].rearrange("p (g t) (c i) -> p g c t i", g=2, i=8),
                 )
             else:
                 for g in halves:
@@ -156,8 +156,8 @@ def tile_softmoe_pb_kernel(tc, h, w2, b2, logits, out):
             eg, el = divmod(e, 4)
             wg = gpool.tile([P, 2, 256, 4], BF16, name="wgs", tag="wgs", align_bytes=64, bufs=2)
             nc.vector.tensor_copy(
-                out=wg[:].rearrange("p g (c i) t -> p g c t i", i=4),
-                in_=wtiles[e][:, :, 256 * dh:256 * (dh + 1)].rearrange("p (g t) (c i) -> p g c t i", g=2, i=4),
+                out=wg[:].rearrange("p g (c i) t -> p g c t i", i=8),
+                in_=wtiles[e][:, :, 256 * dh:256 * (dh + 1)].rearrange("p (g t) (c i) -> p g c t i", g=2, i=8),
             )
             state[("wgs", e, dh)] = wg
 

@@ -17,7 +17,7 @@ NB, NL, ND, NE, NS, NH = 4, 512, 512, 16, 32, 1024
 FLOPS = 2 * NB * NE * NS * NH * ND + 2 * NB * NL * NE * NS * ND
 
 W_BUFS = 5
-S_HALVES = ((1, 1), (5, 1), (9, 1))
+S_HALVES = ((1, 1), (3, 1), (5, 1), (7, 1), (9, 1), (10, 1), (11, 1))
 S_AHEAD = 3
 LAST_SLOT = 2 * 12 + 3
 SPLIT = (12, 13, 14, 15)
@@ -226,16 +226,17 @@ def tile_softmoe_pb_kernel(tc, h, w2, b2, logits, out):
             else:
                 nc.scalar.activation(out=cw[:], in_=state[("ef", b, j)][:], func=ACT.Copy, scale=rinv[:, j:j + 1])
             if j % 2 == 0:
-                state[("cps", b, j // 2)] = psum.tile([P, 2, 4, P], BF16, name="cps", tag="cps")
+                state[("cps", b, j // 2)] = psum.tile([P, 2, 2, P], F32, name="cps", tag="cps")
             cps = state[("cps", b, j // 2)]
-            for t in range(4):
-                nc.tensor.transpose(cps[:, j % 2, t, :], cw[:, t * P:(t + 1) * P], ident_b[:])
+            pairs = cw[:].bitcast(F32)
+            for u in range(2):
+                nc.tensor.transpose(cps[:, j % 2, u, :], pairs[:, u * P:(u + 1) * P], ident_f[:])
 
         def sm_out(b, j):
             if j % 2 == 1:
                 gc = state[("gc", b)]
                 nc.scalar.copy(
-                    out=gc[:, j - 1:j + 1, :, :], in_=state[("cps", b, j // 2)][:].rearrange("p j t l -> p j l t")
+                    out=gc[:, j - 1:j + 1, :, :].bitcast(F32), in_=state[("cps", b, j // 2)][:].rearrange("p j u l -> p j l u")
                 )
 
         def sm_quant(b):
@@ -245,19 +246,20 @@ def tile_softmoe_pb_kernel(tc, h, w2, b2, logits, out):
             )
 
         def eo_tr(b, dh):
-            tps = psum.tile([P, 4, 256], BF16, name="tps", tag=TPS_TAGS[2 * b + dh])
-            for t in range(4):
-                for dl in range(2):
+            tps = psum.tile([P, 2, 256], F32, name="tps", tag=TPS_TAGS[2 * b + dh])
+            for dl in range(2):
+                pairs = eoT[:, 2 * dh + dl, b, :].bitcast(F32)
+                for u in range(2):
                     nc.tensor.transpose(
-                        tps[:, t, dl * P:(dl + 1) * P],
-                        eoT[:, 2 * dh + dl, b, t * P:(t + 1) * P],
-                        ident_b[:],
+                        tps[:, u, dl * P:(dl + 1) * P],
+                        pairs[:, u * P:(u + 1) * P],
+                        ident_f[:],
                     )
             state[("tps", b, dh)] = tps
 
         def eo_out(b, dh):
-            dst = eo_grouped[b][:, 256 * dh:256 * (dh + 1), :]
-            src = state[("tps", b, dh)][:].rearrange("p t d -> p d t")
+            dst = eo_grouped[b][:, 256 * dh:256 * (dh + 1), :].bitcast(F32)
+            src = state[("tps", b, dh)][:].rearrange("p u d -> p d u")
             if dh == 0 or b % 2 == 0:
                 nc.scalar.copy(out=dst, in_=src)
             else:
@@ -381,7 +383,7 @@ def tile_softmoe_pb_kernel(tc, h, w2, b2, logits, out):
                     stage1_out(oe)
 
             tpool = early.enter_context(tc.tile_pool(name="tpool", bufs=1))
-            opool = early.enter_context(tc.tile_pool(name="opool", bufs=3))
+            opool = early.enter_context(tc.tile_pool(name="opool", bufs=6))
             eo_grouped = [shared.tile([P, ND, 4], BF16, name="eo_grouped%d" % b, tag="big", align_bytes=64) for b in range(NB)]
             eo_words = [tpool.tile([P, ND], U32, name="eo_words%d" % b, align_bytes=64) for b in range(NB)]
             eo_scales = [tpool.tile([P, ND], U8, name="eo_scales%d" % b, align_bytes=64) for b in range(NB)]

@@ -17,7 +17,7 @@ NB, NL, ND, NE, NS, NH = 4, 512, 512, 16, 32, 1024
 FLOPS = 2 * NB * NE * NS * NH * ND + 2 * NB * NL * NE * NS * ND
 
 W_BUFS = 5
-S_HALVES = ((1, 1), (3, 1), (5, 1), (7, 1), (9, 1), (10, 1), (11, 1))
+S_HALVES = ()
 S_AHEAD = 3
 LAST_SLOT = 2 * 12 + 3
 SPLIT = (12, 13, 14, 15)

@@ -15,164 +15,121 @@ AXIS = mybir.AxisListType
 P = 128
 NB, NL, ND, NE, NS, NH = 4, 512, 512, 16, 32, 1024
 FLOPS = 2 * NB * NE * NS * NH * ND + 2 * NB * NL * NE * NS * ND
+DH = 256
 
-W_BUFS = 5
-S_HALVES = ()
-S_AHEAD = 3
-LAST_SLOT = 2 * 12 + 3
-SPLIT = (12, 13, 14, 15)
-SCALE_ON_VECTOR = ()
-TPS_TAGS = ("tr", "ps1", "tr", "ps1", "tr", "ps1", "tr", "ps1")
+E_SPLIT = 8
+UNITS = [(e, dh) for e in range(E_SPLIT) for dh in range(2)] + [(e, dh) for dh in range(2) for e in range(E_SPLIT, NE)]
+NU = len(UNITS)
+ON_SCALAR = (10, 16, 22)
+S_AHEAD = 2
 
 
 def tile_softmoe_pb_kernel(tc, h, w2, b2, logits, out):
     nc = tc.nc
     with ExitStack() as ctx:
         const = ctx.enter_context(tc.tile_pool(name="const", bufs=1))
+        shared = ctx.enter_context(tc.tile_pool(name="shared", bufs=4))
         smpool = ctx.enter_context(tc.tile_pool(name="smpool", bufs=2))
-        epool = ctx.enter_context(tc.tile_pool(name="epool", bufs=5))
+        epool = ctx.enter_context(tc.tile_pool(name="epool", bufs=4))
+        hpool = ctx.enter_context(tc.tile_pool(name="hpool", bufs=2))
+        wpool = ctx.enter_context(tc.tile_pool(name="wpool", bufs=8))
+        gpool = ctx.enter_context(tc.tile_pool(name="gpool", bufs=4))
+        cpool = ctx.enter_context(tc.tile_pool(name="cpool", bufs=4))
+        opool = ctx.enter_context(tc.tile_pool(name="opool", bufs=8))
         psum = ctx.enter_context(tc.psum_pool(name="psum", bufs=2))
 
+        zero = const.tile([P, 1], F32, name="zero")
+        warm = const.tile([P, 1], F32, name="warm")
         ident_f = const.tile([P, P], F32, name="ident_f")
         make_identity(nc, ident_f[:])
         ident_b = const.tile([P, P], BF16, name="ident_b")
         make_identity(nc, ident_b[:])
-
         h_words = [const.tile([P, 1024], U32, name="h_words%d" % eg, align_bytes=64) for eg in range(4)]
         h_scales = [const.tile([P, 1024], U8, name="h_scales%d" % eg, align_bytes=64) for eg in range(4)]
         cw_words = [const.tile([P, NL], U32, name="cw_words%d" % b, align_bytes=64) for b in range(NB)]
         cw_scales = [const.tile([P, NL], U8, name="cw_scales%d" % b, align_bytes=64) for b in range(NB)]
-        shared = ctx.enter_context(tc.tile_pool(name="shared", bufs=4))
+        eo_words = [const.tile([P, ND], U32, name="eo_words%d" % b, align_bytes=64) for b in range(NB)]
+        eo_scales = [const.tile([P, ND], U8, name="eo_scales%d" % b, align_bytes=64) for b in range(NB)]
         lraw = [shared.tile([P, 4, 512], BF16, name="lraw%d" % b, tag="big", align_bytes=64) for b in range(NB)]
         eoT = const.tile([P, 4, NB, 512], BF16, name="eoT")
         b2z = const.tile([P, ND], BF16, name="b2z")
         b2T = const.tile([P, 4, NE], F32, name="b2T")
-
-        wtiles = {}
-        htiles = {}
         state = {}
 
         def load_w(e):
             wraw = wpool.tile([P, 8, ND], BF16, name="wraw", tag="wraw")
             src = w2[e].rearrange("(c p r) d -> p c (r d)", c=4, p=P, r=2)
-            dst = wraw[:].rearrange("p (c r) d -> p c (r d)", c=4, r=2)
-            nc.sync.dma_start(out=dst, in_=src)
-            wtiles[e] = wraw
+            nc.sync.dma_start(out=wraw[:].rearrange("p (c r) d -> p c (r d)", c=4, r=2), in_=src)
+            state["w", e] = wraw
 
         def load_h(eg):
+            hraw = hpool.tile([P, NB, NH], BF16, name="hraw", tag="hraw")
             for b in range(NB):
-                hraw = hpool.tile([P, NH], BF16, name="hraw", tag="hraw")
-                nc.sync.dma_start(out=hraw[:], in_=h[b, 4 * eg:4 * eg + 4].rearrange("e s k -> (e s) k"))
-                htiles[(eg, b)] = hraw
+                nc.sync.dma_start(out=hraw[:, b, :], in_=h[b, 4 * eg:4 * eg + 4].rearrange("e s k -> (e s) k"))
+            state["h", eg] = hraw
+
+        def load_b2():
+            nc.sync.dma_start(out=b2z[0:NE, :], in_=b2)
 
         def load_logits(b):
             nc.sync.dma_start(out=lraw[b][:], in_=logits[b].rearrange("(p j) e s -> p j (e s)", j=4))
 
-        def h_tile(eg, b):
+        def h_tr(eg, b):
             if b == 0:
-                state[("gh", eg)] = ghpool.tile([P, 4096], BF16, name="gh", tag="gh", align_bytes=64)
-            gh = state[("gh", eg)]
-            gh32 = gh[:].bitcast(F32).rearrange("p (a b s u) -> p a b s u", a=8, b=NB, s=NS, u=2)
+                state["gh", eg] = hpool.tile([P, 4096], BF16, name="gh", tag="gh", align_bytes=64)
             hps = psum.tile([P, 2, 8, NS], F32, name="hps", tag="tr")
-            words = htiles[(eg, b)][:].bitcast(F32)
+            words = state["h", eg][:, b, :].bitcast(F32)
             for g in range(2):
                 for u in range(2):
                     c = 2 * g + u
                     nc.tensor.transpose(
-                        hps[:, u, 4 * g:4 * g + 4, :].rearrange("p e s -> p (e s)"),
-                        words[:, c * P:(c + 1) * P],
-                        ident_f[:],
+                        hps[:, u, 4 * g:4 * g + 4, :].rearrange("p e s -> p (e s)"), words[:, c * P:(c + 1) * P], ident_f[:]
                     )
-            nc.scalar.copy(out=gh32[:, :, b, :, :], in_=hps[:].rearrange("p u a s -> p a s u"))
+            state["hps", eg, b] = hps
+
+        def h_out(eg, b):
+            gh32 = state["gh", eg][:].bitcast(F32).rearrange("p (a b s u) -> p a b s u", a=8, b=NB, s=NS, u=2)
+            nc.scalar.copy(out=gh32[:, :, b, :, :], in_=state["hps", eg, b][:].rearrange("p u a s -> p a s u"))
 
         def h_quant(eg):
-            nc.vector.quantize_mx(out=h_words[eg][:].bitcast(FP8X4), scales=h_scales[eg][:], in_=state[("gh", eg)][:])
+            nc.vector.quantize_mx(out=h_words[eg][:].bitcast(FP8X4), scales=h_scales[eg][:], in_=state["gh", eg][:])
 
-        def grouped_tile(e):
-            if ("wg", e) not in state:
-                state[("wg", e)] = gpool.tile([P, 2, ND, 4], BF16, name="wg", tag="wg", align_bytes=64)
-            return state[("wg", e)]
+        def unit_tile(i):
+            if ("wg", i) not in state:
+                state["wg", i] = gpool.tile([P, 2, DH, 4], BF16, name="wg", tag="wg", align_bytes=64)
+            return state["wg", i]
 
-        def regroup_half(e, g, on_scalar):
-            wg = grouped_tile(e)
-            dst = wg[:, g, :, :].rearrange("p (c i) t -> p c t i", i=8)
-            src = wtiles[e][:, 4 * g:4 * g + 4, :].rearrange("p t (c i) -> p c t i", i=8)
+        def regroup(i, on_scalar):
+            e, dh = UNITS[i]
+            wg = unit_tile(i)
+            src = state["w", e][:, :, DH * dh:DH * (dh + 1)]
             if on_scalar:
-                nc.scalar.copy(out=dst, in_=src)
-            else:
-                nc.vector.tensor_copy(out=dst, in_=src)
-
-        def regroup_vector(e):
-            halves = [g for g in range(2) if (e, g) not in S_HALVES]
-            if len(halves) == 2:
-                wg = grouped_tile(e)
+                nc.scalar.copy(
+                    out=wg[:, 1, :, :].rearrange("p (c i) t -> p c t i", i=8), in_=src[:, 4:8, :].rearrange("p t (c i) -> p c t i", i=8)
+                )
+            elif i in ON_SCALAR:
                 nc.vector.tensor_copy(
-                    out=wg[:].rearrange("p g (c i) t -> p g c t i", i=8),
-                    in_=wtiles[e][:].rearrange("p (g t) (c i) -> p g c t i", g=2, i=8),
+                    out=wg[:, 0, :, :].rearrange("p (c i) t -> p c t i", i=8), in_=src[:, 0:4, :].rearrange("p t (c i) -> p c t i", i=8)
                 )
             else:
-                for g in halves:
-                    regroup_half(e, g, False)
-
-        def quant_w(e):
-            ww = cpool.tile([P, 2 * ND], U32, name="ww", tag="ww", align_bytes=64)
-            ws = cpool.tile([P, 2 * ND], U8, name="ws", tag="ws", align_bytes=64)
-            nc.vector.quantize_mx(
-                out=ww[:].bitcast(FP8X4), scales=ws[:], in_=state[("wg", e)][:].rearrange("p g d t -> p (g d t)")
-            )
-            state[("codes", e)] = (ww, ws)
-
-        def stage1_mm(e):
-            eg, el = divmod(e, 4)
-            ps1 = psum.tile([P, 4, P], F32, name="ps1", tag="ps1")
-            ww, ws = state[("codes", e)]
-            for dc in range(4):
-                for g in range(2):
-                    a = 4 * g + el
-                    c0 = g * ND + dc * P
-                    nc.tensor.matmul_mx(
-                        out=ps1[:, dc, :],
-                        lhsT=ww[:, c0:c0 + P].bitcast(FP8X4),
-                        lhsT_scale=ws[:, c0:c0 + P],
-                        rhs=h_words[eg][:, a * P:(a + 1) * P].bitcast(FP8X4),
-                        rhs_scale=h_scales[eg][:, a * P:(a + 1) * P],
-                        start=(g == 0),
-                        stop=(g == 1),
-                    )
-            state[("ps1", e)] = ps1
-
-        def stage1_out(e):
-            ps1 = state[("ps1", e)]
-            for dc in range(4):
-                nc.scalar.activation(
-                    out=eoT[:, dc, :, NS * e:NS * (e + 1)],
-                    in_=ps1[:, dc, :].rearrange("p (b s) -> p b s", b=NB),
-                    func=ACT.Identity,
-                    bias=b2T[:, dc, e:e + 1],
-                    scale=1.0,
+                nc.vector.tensor_copy(
+                    out=wg[:].rearrange("p g (c i) t -> p g c t i", i=8), in_=src.rearrange("p (g t) (c i) -> p g c t i", g=2, i=8)
                 )
 
-        def split_unit(e, dh):
-            eg, el = divmod(e, 4)
-            wg = gpool.tile([P, 2, 256, 4], BF16, name="wgs", tag="wgs", align_bytes=64, bufs=2)
-            nc.vector.tensor_copy(
-                out=wg[:].rearrange("p g (c i) t -> p g c t i", i=8),
-                in_=wtiles[e][:, :, 256 * dh:256 * (dh + 1)].rearrange("p (g t) (c i) -> p g c t i", g=2, i=8),
-            )
-            state[("wgs", e, dh)] = wg
+        def unit_quant(i):
+            ww = cpool.tile([P, 2 * DH], U32, name="ww", tag="ww", align_bytes=64)
+            ws = cpool.tile([P, 2 * DH], U8, name="ws", tag="ws", align_bytes=64)
+            nc.vector.quantize_mx(out=ww[:].bitcast(FP8X4), scales=ws[:], in_=state["wg", i][:].rearrange("p g d t -> p (g d t)"))
+            state["codes", i] = (ww, ws)
 
-        def split_quant(e, dh):
-            eg, el = divmod(e, 4)
-            ww = cpool.tile([P, ND], U32, name="wws", tag="wws", align_bytes=64, bufs=2)
-            ws = cpool.tile([P, ND], U8, name="wss", tag="wss", align_bytes=64, bufs=2)
-            nc.vector.quantize_mx(
-                out=ww[:].bitcast(FP8X4), scales=ws[:], in_=state[("wgs", e, dh)][:].rearrange("p g d t -> p (g d t)")
-            )
-            ps1 = psum.tile([P, 2, P], F32, name="ps1", tag="ps1")
+        def unit_mm(i):
+            eg, el = divmod(UNITS[i][0], 4)
+            ww, ws = state["codes", i]
+            ps1 = psum.tile([P, 4, P], F32, name="ps1", tag="ps1")
             for dl in range(2):
                 for g in range(2):
+                    c0 = g * DH + dl * P
                     a = 4 * g + el
-                    c0 = g * 256 + dl * P
                     nc.tensor.matmul_mx(
                         out=ps1[:, dl, :],
                         lhsT=ww[:, c0:c0 + P].bitcast(FP8X4),
@@ -182,12 +139,17 @@ def tile_softmoe_pb_kernel(tc, h, w2, b2, logits, out):
                         start=(g == 0),
                         stop=(g == 1),
                     )
+            state["ps1", i] = ps1
+
+        def unit_out(i):
+            e, dh = UNITS[i]
             for dl in range(2):
+                dc = 2 * dh + dl
                 nc.scalar.activation(
-                    out=eoT[:, 2 * dh + dl, :, NS * e:NS * (e + 1)],
-                    in_=ps1[:, dl, :].rearrange("p (b s) -> p b s", b=NB),
+                    out=eoT[:, dc, :, NS * e:NS * (e + 1)],
+                    in_=state["ps1", i][:, dl, :].rearrange("p (b s) -> p b s", b=NB),
                     func=ACT.Identity,
-                    bias=b2T[:, 2 * dh + dl, e:e + 1],
+                    bias=b2T[:, dc, e:e + 1],
                     scale=1.0,
                 )
 
@@ -201,200 +163,183 @@ def tile_softmoe_pb_kernel(tc, h, w2, b2, logits, out):
             nc.vector.tensor_reduce(out=mx[:], in_=m2[:], axis=AXIS.X, op=ALU.max)
             nmax = smpool.tile([P, 4], F32, name="nmax", tag="nmax")
             nc.vector.tensor_scalar(out=nmax[:], in0=mx[:], scalar1=-1.0, scalar2=None, op0=ALU.mult)
-            state[("nmax", b)] = nmax
-            state[("ssum", b)] = smpool.tile([P, 4], F32, name="ssum", tag="ssum")
-            state[("gc", b)] = smpool.tile([P, 4, P, 4], BF16, name="gc", tag="gc", align_bytes=64)
+            state["nmax", b] = nmax
+            state["ssum", b] = smpool.tile([P, 4], F32, name="ssum", tag="ssum")
 
         def sm_exp(b, j):
             ef = epool.tile([P, 512], F32, name="ef", tag="ef")
             nc.scalar.activation(
                 out=ef[:], in_=lraw[b][:, j, :], func=ACT.Exp,
-                bias=state[("nmax", b)][:, j:j + 1], scale=1.0, accum_out=state[("ssum", b)][:, j:j + 1],
+                bias=state["nmax", b][:, j:j + 1], scale=1.0, accum_out=state["ssum", b][:, j:j + 1],
             )
-            state[("ef", b, j)] = ef
+            state["ef", b, j] = ef
 
         def sm_norm(b):
             rinv = smpool.tile([P, 4], F32, name="rinv", tag="rinv")
-            nc.vector.reciprocal(out=rinv[:], in_=state[("ssum", b)][:])
-            state[("rinv", b)] = rinv
+            nc.vector.reciprocal(out=rinv[:], in_=state["ssum", b][:])
+            state["rinv", b] = rinv
+            state["gc", b] = smpool.tile([P, 4, P, 4], BF16, name="gc", tag="gc", align_bytes=64)
 
         def sm_tr(b, j):
-            cw = epool.tile([P, 512], BF16, name="cw", tag="cw", bufs=3)
-            rinv = state[("rinv", b)]
-            if j in SCALE_ON_VECTOR:
-                nc.vector.tensor_scalar(out=cw[:], in0=state[("ef", b, j)][:], scalar1=rinv[:, j:j + 1], scalar2=None, op0=ALU.mult)
-            else:
-                nc.scalar.activation(out=cw[:], in_=state[("ef", b, j)][:], func=ACT.Copy, scale=rinv[:, j:j + 1])
+            cw = epool.tile([P, 512], BF16, name="cw", tag="cw")
+            nc.scalar.activation(out=cw[:], in_=state["ef", b, j][:], func=ACT.Copy, scale=state["rinv", b][:, j:j + 1])
             if j % 2 == 0:
-                state[("cps", b, j // 2)] = psum.tile([P, 2, 2, P], F32, name="cps", tag="cps")
-            cps = state[("cps", b, j // 2)]
+                state["cps", b, j // 2] = psum.tile([P, 2, 2, P], F32, name="cps", tag="cps")
             pairs = cw[:].bitcast(F32)
             for u in range(2):
-                nc.tensor.transpose(cps[:, j % 2, u, :], pairs[:, u * P:(u + 1) * P], ident_f[:])
+                nc.tensor.transpose(state["cps", b, j // 2][:, j % 2, u, :], pairs[:, u * P:(u + 1) * P], ident_f[:])
 
-        def sm_out(b, j):
-            if j % 2 == 1:
-                gc = state[("gc", b)]
-                nc.scalar.copy(
-                    out=gc[:, j - 1:j + 1, :, :].bitcast(F32), in_=state[("cps", b, j // 2)][:].rearrange("p j u l -> p j l u")
-                )
+        def sm_out(b, jp):
+            nc.scalar.copy(
+                out=state["gc", b][:, 2 * jp:2 * jp + 2, :, :].bitcast(F32), in_=state["cps", b, jp][:].rearrange("p j u l -> p j l u")
+            )
 
         def sm_quant(b):
             nc.vector.quantize_mx(
-                out=cw_words[b][:].bitcast(FP8X4), scales=cw_scales[b][:],
-                in_=state[("gc", b)][:].rearrange("p j l t -> p (j l t)"),
+                out=cw_words[b][:].bitcast(FP8X4), scales=cw_scales[b][:], in_=state["gc", b][:].rearrange("p j l t -> p (j l t)")
             )
 
         def eo_tr(b, dh):
-            tps = psum.tile([P, 2, 256], F32, name="tps", tag=TPS_TAGS[2 * b + dh])
+            tps = psum.tile([P, 2, DH], F32, name="tps", tag=("tr", "tr", "ps1", "ps1")[b] if dh == 1 else "tr")
             for dl in range(2):
                 pairs = eoT[:, 2 * dh + dl, b, :].bitcast(F32)
                 for u in range(2):
-                    nc.tensor.transpose(
-                        tps[:, u, dl * P:(dl + 1) * P],
-                        pairs[:, u * P:(u + 1) * P],
-                        ident_f[:],
-                    )
-            state[("tps", b, dh)] = tps
+                    nc.tensor.transpose(tps[:, u, dl * P:(dl + 1) * P], pairs[:, u * P:(u + 1) * P], ident_f[:])
+            state["tps", b] = tps
 
-        def eo_out(b, dh):
-            dst = eo_grouped[b][:, 256 * dh:256 * (dh + 1), :].bitcast(F32)
-            src = state[("tps", b, dh)][:].rearrange("p u d -> p d u")
-            if dh == 0 or b % 2 == 0:
-                nc.scalar.copy(out=dst, in_=src)
-            else:
+        def eo_out(b, dh, on_vector):
+            if dh == 0:
+                state["eo", b] = shared.tile([P, ND, 4], BF16, name="eo", tag="big", align_bytes=64)
+            dst = state["eo", b][:, DH * dh:DH * (dh + 1), :].bitcast(F32)
+            src = state["tps", b][:].rearrange("p u d -> p d u")
+            if on_vector:
                 nc.vector.tensor_copy(out=dst, in_=src)
+            else:
+                nc.scalar.copy(out=dst, in_=src)
 
         def eo_quant(b, dh):
+            cols = slice(DH * dh, DH * (dh + 1))
             nc.vector.quantize_mx(
-                out=eo_words[b][:, 256 * dh:256 * (dh + 1)].bitcast(FP8X4), scales=eo_scales[b][:, 256 * dh:256 * (dh + 1)],
-                in_=eo_grouped[b][:, 256 * dh:256 * (dh + 1), :].rearrange("p d t -> p (d t)"),
+                out=eo_words[b][:, cols].bitcast(FP8X4), scales=eo_scales[b][:, cols], in_=state["eo", b][:, cols, :].rearrange("p d t -> p (d t)")
             )
 
-        def combine(b, dh):
-            ob = opool.tile([P, 4, 256], F32, name="ob", tag="ob")
+        def combine_mm(b, dh):
+            cols = slice(DH * dh, DH * (dh + 1))
             for jp in range(2):
-                ps2 = psum.tile([P, 2, 256], F32, name="ps2", tag=("ps2", "cps")[jp])
+                ps2 = psum.tile([P, 2, DH], F32, name="ps2", tag=("ps2", "cps")[jp])
                 for jj in range(2):
                     j = 2 * jp + jj
                     nc.tensor.matmul_mx(
                         out=ps2[:, jj, :],
                         lhsT=cw_words[b][:, j * P:(j + 1) * P].bitcast(FP8X4),
                         lhsT_scale=cw_scales[b][:, j * P:(j + 1) * P],
-                        rhs=eo_words[b][:, 256 * dh:256 * (dh + 1)].bitcast(FP8X4),
-                        rhs_scale=eo_scales[b][:, 256 * dh:256 * (dh + 1)],
+                        rhs=eo_words[b][:, cols].bitcast(FP8X4),
+                        rhs_scale=eo_scales[b][:, cols],
                         start=True,
                         stop=True,
                     )
-                if jp == 0 or (dh == 0 and b < 1):
-                    nc.scalar.copy(out=ob[:, 2 * jp:2 * jp + 2, :], in_=ps2[:])
-                else:
-                    nc.vector.tensor_copy(out=ob[:, 2 * jp:2 * jp + 2, :], in_=ps2[:])
-            dram = out[b].rearrange("(p j) d -> p j d", j=4)
-            nc.sync.dma_start(out=dram[:, :, 256 * dh:256 * (dh + 1)], in_=ob[:])
+                state["ps2", b, jp] = ps2
 
-        def bias_tr():
+        def combine_out(b, dh, jp, on_vector):
+            ob = opool.tile([P, 2, DH], F32, name="ob", tag="ob")
+            if on_vector:
+                nc.vector.tensor_copy(out=ob[:], in_=state["ps2", b, jp][:])
+            else:
+                nc.scalar.copy(out=ob[:], in_=state["ps2", b, jp][:])
+            dram = out[b].rearrange("(p j) d -> p j d", j=4)
+            nc.sync.dma_start(out=dram[:, 2 * jp:2 * jp + 2, DH * dh:DH * (dh + 1)], in_=ob[:])
+
+        def bias():
             bps = psum.tile([P, 4, P], BF16, name="bps", tag="ps2")
             for dc in range(4):
                 nc.tensor.transpose(bps[:, dc, :], b2z[:, dc * P:(dc + 1) * P], ident_b[:])
-            state["bps"] = bps
-
-        def bias_out():
-            nc.vector.tensor_copy(out=b2T[:], in_=state["bps"][:, :, 0:NE])
+            nc.vector.tensor_copy(out=b2T[:], in_=bps[:, :, 0:NE])
 
         extras = {}
 
         def at(slot, fn, *args):
             extras[slot] = extras.get(slot, []) + [(fn, args)]
 
-        def plan_softmax(b, s_max, s_exp, s_norm, s_q):
-            at(s_max, sm_max, b)
+        for b, s0 in enumerate((-2, 5, 11, 17)):
+            if b > 1:
+                at(s0, sm_max, b)
             for j in range(4):
-                at(s_exp[j], sm_exp, b, j)
-            at(s_norm, sm_norm, b)
+                at(max(s0 + 1 + j, 0) if b else 0, sm_exp, b, j)
+            at(s0 + 5, sm_norm, b)
             for j in range(4):
-                at(s_norm + j, sm_tr, b, j)
-                at(s_norm + j + 1, sm_out, b, j)
-            at(s_q, sm_quant, b)
-
-        def softmax_all(b):
-            sm_max(b)
-            for j in range(4):
-                sm_exp(b, j)
-            sm_norm(b)
-            for j in range(4):
-                sm_tr(b, j)
-                sm_out(b, j)
-            sm_quant(b)
-
-        plan_softmax(0, -2, (-2, -2, -2, -2), 1, 7)
-        plan_softmax(1, 1, (1, 1, 2, 2), 5, 11)
-        plan_softmax(2, 12, (13, 14, 15, 16), 18, 24)
-        plan_softmax(3, 17, (18, 19, 20, 21), 22, 27)
-        at(-2, bias_tr)
-        for b in range(NB):
-            at(-1, h_tile, 0, b)
-        at(3, bias_out)
-        at(2, h_quant, 0)
-        for eg in range(1, 4):
+                at(s0 + 5 + j // 2, sm_tr, b, j)
+            at(s0 + 6, sm_out, b, 0)
+            at(s0 + 7, sm_out, b, 1)
+            at(s0 + 9, sm_quant, b)
+        at(1, sm_max, 1)
+        at(0, bias)
+        for b in range(2):
+            at(0, h_tr, 0, b)
+            at(1, h_out, 0, b)
+        for b in range(2, 4):
+            at(1, h_tr, 0, b)
+            at(2, h_out, 0, b)
+        at(3, h_quant, 0)
+        for eg, s0 in ((1, 2), (2, 5), (3, 11)):
             for b in range(NB):
-                at(8 * eg - 4 + b, h_tile, eg, b)
-            at(8 * eg + 1, h_quant, eg)
-        at(0, load_h, 1)
-        at(2, load_logits, 3)
-        at(8, load_h, 2)
-        at(16, load_h, 3)
+                at(s0 + b, h_tr, eg, b)
+                at(s0 + b + 1, h_out, eg, b)
+            at(s0 + 6, h_quant, eg)
+        for b in range(NB):
+            at(26 + b, eo_out, b, 0, False)
+            at(27 + b, eo_quant, b, 0)
+            at(27 + b, combine_mm, b, 0)
+            for jp in range(2):
+                if b < 3:
+                    at(28 + b, combine_out, b, 0, jp, False)
+        loads = {2: [(load_h, 2), (load_w, 4), (load_w, 5), (load_logits, 2), (load_w, 6)], 6: [(load_h, 3), (load_w, 7), (load_w, 8), (load_w, 9)],
+                 7: [(load_w, 10), (load_logits, 3)]}
+        for e in range(11, NE):
+            loads[2 * (e - E_SPLIT) + 2] = [(load_w, e)]
 
-        with ExitStack() as early:
-            hpool = early.enter_context(tc.tile_pool(name="hpool", bufs=4))
-            ghpool = early.enter_context(tc.tile_pool(name="ghpool", bufs=1))
-            wpool = early.enter_context(tc.tile_pool(name="wpool", bufs=W_BUFS))
-            gpool = early.enter_context(tc.tile_pool(name="gpool", bufs=3))
-            cpool = early.enter_context(tc.tile_pool(name="cpool", bufs=3))
-
+        with tc.manual_schedule():
+            nc.vector.memset(zero[:], 0.0)
+            nc.scalar.activation(out=warm[:], in_=zero[:], func=ACT.Exp)
             nc.vector.memset(b2z[:], 0.0)
-            load_logits(0)
-            nc.sync.dma_start(out=b2z[0:NE, :], in_=b2)
-            load_w(0)
-            load_logits(1)
-            load_w(1)
-            load_h(0)
-            load_w(2)
-            load_w(3)
-            load_logits(2)
-
-            for s in range(-2, LAST_SLOT + 1):
-                e = s // 2
-                if 0 <= s < 2 * NE and s % 2 == 0 and e + W_BUFS - 1 < NE:
-                    load_w(e + W_BUFS - 1)
-                for (se, sg) in S_HALVES:
-                    if 2 * se - S_AHEAD == s:
-                        regroup_half(se, sg, True)
-                if 0 <= s < 2 * NE and s % 2 == 0 and e not in SPLIT:
-                    regroup_vector(e)
-                qe = (s - 3) // 2 if s % 2 == 1 else -1
-                if 0 <= qe < NE and qe not in SPLIT:
-                    quant_w(qe)
-                    stage1_mm(qe)
+            for fn, args in ((load_logits, (0,)), (load_b2, ()), (load_w, (0,)), (load_logits, (1,)), (load_w, (1,)), (load_h, (0,)), (load_w, (2,)),
+                             (load_h, (1,)), (load_w, (3,)), (sm_max, (0,))):
+                fn(*args)
+            for s in range(NU + 2):
+                if s + S_AHEAD in ON_SCALAR:
+                    regroup(s + S_AHEAD, True)
+                if s < NU:
+                    regroup(s, False)
+                for fn, args in loads.get(s, []):
+                    fn(args)
                 for fn, args in extras.get(s, []):
                     fn(*args)
-                oe = (s - 4) // 2 if s % 2 == 0 else -1
-                if 0 <= oe < NE and oe not in SPLIT:
-                    stage1_out(oe)
-
-            tpool = early.enter_context(tc.tile_pool(name="tpool", bufs=1))
-            opool = early.enter_context(tc.tile_pool(name="opool", bufs=6))
-            eo_grouped = [shared.tile([P, ND, 4], BF16, name="eo_grouped%d" % b, tag="big", align_bytes=64) for b in range(NB)]
-            eo_words = [tpool.tile([P, ND], U32, name="eo_words%d" % b, align_bytes=64) for b in range(NB)]
-            eo_scales = [tpool.tile([P, ND], U8, name="eo_scales%d" % b, align_bytes=64) for b in range(NB)]
-            for dh in range(2):
-                for k in range(len(SPLIT) + 1):
-                    if k < len(SPLIT):
-                        split_unit(SPLIT[k], dh)
-                    if k >= 1:
-                        split_quant(SPLIT[k - 1], dh)
-                for b in range(NB):
-                    eo_tr(b, dh)
-                    eo_out(b, dh)
-                    eo_quant(b, dh)
-                    combine(b, dh)
+                if s >= 5:
+                    unit_out(s - 2)
+                if 25 <= s < 25 + NB:
+                    eo_tr(s - 25, 0)
+                if 1 <= s <= NU:
+                    unit_quant(s - 1)
+                if s == 3:
+                    unit_mm(0)
+                    unit_mm(1)
+                    unit_out(0)
+                    unit_mm(2)
+                elif s == 4:
+                    unit_out(1)
+                    unit_mm(3)
+                    unit_out(2)
+                elif 5 <= s <= NU:
+                    unit_mm(s - 1)
+            for jp in range(2):
+                combine_out(3, 0, jp, True)
+            for b in range(NB):
+                eo_tr(b, 1)
+            for k in range(NB + 2):
+                if k < NB:
+                    eo_out(k, 1, k == 1)
+                if 1 <= k <= NB:
+                    eo_quant(k - 1, 1)
+                    combine_mm(k - 1, 1)
+                if k >= 2:
+                    combine_out(k - 2, 1, 0, True)
+                    combine_out(k - 2, 1, 1, False)

@@ -20,7 +20,7 @@ DH = 256
 E_SPLIT = 8
 UNITS = [(e, dh) for e in range(E_SPLIT) for dh in range(2)] + [(e, dh) for dh in range(2) for e in range(E_SPLIT, NE)]
 NU = len(UNITS)
-ON_SCALAR = (10, 16, 22)
+ON_SCALAR = ()
 S_AHEAD = 2
 
 
@@ -279,12 +279,12 @@ def tile_softmoe_pb_kernel(tc, h, w2, b2, logits, out):
         for b in range(2, 4):
             at(1, h_tr, 0, b)
             at(2, h_out, 0, b)
-        at(3, h_quant, 0)
-        for eg, s0 in ((1, 2), (2, 5), (3, 11)):
+        at(4, h_quant, 0)
+        for eg, s0 in ((1, 2), (2, 6), (3, 12)):
             for b in range(NB):
                 at(s0 + b, h_tr, eg, b)
                 at(s0 + b + 1, h_out, eg, b)
-            at(s0 + 6, h_quant, eg)
+            at(s0 + 7, h_quant, eg)
         for b in range(NB):
             at(26 + b, eo_out, b, 0, False)
             at(27 + b, eo_quant, b, 0)
@@ -292,7 +292,7 @@ def tile_softmoe_pb_kernel(tc, h, w2, b2, logits, out):
             for jp in range(2):
                 if b < 3:
                     at(28 + b, combine_out, b, 0, jp, False)
-        loads = {2: [(load_h, 2), (load_w, 4), (load_w, 5), (load_logits, 2), (load_w, 6)], 6: [(load_h, 3), (load_w, 7), (load_w, 8), (load_w, 9)],
+        loads = {2: [(load_w, 4), (load_h, 2), (load_w, 5), (load_logits, 2), (load_w, 6)], 6: [(load_w, 7), (load_h, 3), (load_w, 8), (load_w, 9)],
                  7: [(load_w, 10), (load_logits, 3)]}
         for e in range(11, NE):
             loads[2 * (e - E_SPLIT) + 2] = [(load_w, e)]
@@ -319,12 +319,11 @@ def tile_softmoe_pb_kernel(tc, h, w2, b2, logits, out):
                     eo_tr(s - 25, 0)
                 if 1 <= s <= NU:
                     unit_quant(s - 1)
-                if s == 3:
+                if s == 4:
                     unit_mm(0)
                     unit_mm(1)
                     unit_out(0)
                     unit_mm(2)
-                elif s == 4:
                     unit_out(1)
                     unit_mm(3)
                     unit_out(2)

@@ -18,17 +18,17 @@ FLOPS = 2 * NB * NE * NS * NH * ND + 2 * NB * NL * NE * NS * ND
 DH = 256
 
 E_SPLIT = 8
-UNITS = [(e, dh) for e in range(E_SPLIT) for dh in range(2)] + [(e, dh) for dh in range(2) for e in range(E_SPLIT, NE)]
+PARTS = ((0, 256), (256, 128), (384, 128))
+UNITS = [(e, d0, DH) for e in range(E_SPLIT) for d0 in (0, DH)] + [(e, d0, width) for d0, width in PARTS for e in range(E_SPLIT, NE)]
 NU = len(UNITS)
-ON_SCALAR = ()
-S_AHEAD = 2
+ON_SCALAR = (8, 11, 14, 17, 20)
 
 
 def tile_softmoe_pb_kernel(tc, h, w2, b2, logits, out):
     nc = tc.nc
     with ExitStack() as ctx:
         const = ctx.enter_context(tc.tile_pool(name="const", bufs=1))
-        shared = ctx.enter_context(tc.tile_pool(name="shared", bufs=4))
+        shared = ctx.enter_context(tc.tile_pool(name="shared", bufs=2))
         smpool = ctx.enter_context(tc.tile_pool(name="smpool", bufs=2))
         epool = ctx.enter_context(tc.tile_pool(name="epool", bufs=4))
         hpool = ctx.enter_context(tc.tile_pool(name="hpool", bufs=2))
@@ -50,7 +50,7 @@ def tile_softmoe_pb_kernel(tc, h, w2, b2, logits, out):
         cw_scales = [const.tile([P, NL], U8, name="cw_scales%d" % b, align_bytes=64) for b in range(NB)]
         eo_words = [const.tile([P, ND], U32, name="eo_words%d" % b, align_bytes=64) for b in range(NB)]
         eo_scales = [const.tile([P, ND], U8, name="eo_scales%d" % b, align_bytes=64) for b in range(NB)]
-        lraw = [shared.tile([P, 4, 512], BF16, name="lraw%d" % b, tag="big", align_bytes=64) for b in range(NB)]
+        lraw = [shared.tile([P, 8, 512], BF16, name="lraw%d" % q, tag="big", align_bytes=64) for q in range(2)]
         eoT = const.tile([P, 4, NB, 512], BF16, name="eoT")
         b2z = const.tile([P, ND], BF16, name="b2z")
         b2T = const.tile([P, 4, NE], F32, name="b2T")
@@ -72,7 +72,8 @@ def tile_softmoe_pb_kernel(tc, h, w2, b2, logits, out):
             nc.sync.dma_start(out=b2z[0:NE, :], in_=b2)
 
         def load_logits(b):
-            nc.sync.dma_start(out=lraw[b][:], in_=logits[b].rearrange("(p j) e s -> p j (e s)", j=4))
+            q, r = divmod(b, 2)
+            nc.sync.dma_start(out=lraw[q][:, 4 * r:4 * r + 4, :], in_=logits[b].rearrange("(p j) e s -> p j (e s)", j=4))
 
         def h_tr(eg, b):
             if b == 0:
@@ -94,20 +95,16 @@ def tile_softmoe_pb_kernel(tc, h, w2, b2, logits, out):
         def h_quant(eg):
             nc.vector.quantize_mx(out=h_words[eg][:].bitcast(FP8X4), scales=h_scales[eg][:], in_=state["gh", eg][:])
 
-        def unit_tile(i):
+        def group_tile(i):
             if ("wg", i) not in state:
-                state["wg", i] = gpool.tile([P, 2, DH, 4], BF16, name="wg", tag="wg", align_bytes=64)
+                state["wg", i] = gpool.tile([P, 2, UNITS[i][2], 4], BF16, name="wg", tag="wg", align_bytes=64)
             return state["wg", i]
 
-        def regroup(i, on_scalar):
-            e, dh = UNITS[i]
-            wg = unit_tile(i)
-            src = state["w", e][:, :, DH * dh:DH * (dh + 1)]
-            if on_scalar:
-                nc.scalar.copy(
-                    out=wg[:, 1, :, :].rearrange("p (c i) t -> p c t i", i=8), in_=src[:, 4:8, :].rearrange("p t (c i) -> p c t i", i=8)
-                )
-            elif i in ON_SCALAR:
+        def regroup(i):
+            e, d0, width = UNITS[i]
+            wg = group_tile(i)
+            src = state["w", e][:, :, d0:d0 + width]
+            if i in ON_SCALAR:
                 nc.vector.tensor_copy(
                     out=wg[:, 0, :, :].rearrange("p (c i) t -> p c t i", i=8), in_=src[:, 0:4, :].rearrange("p t (c i) -> p c t i", i=8)
                 )
@@ -116,19 +113,28 @@ def tile_softmoe_pb_kernel(tc, h, w2, b2, logits, out):
                     out=wg[:].rearrange("p g (c i) t -> p g c t i", i=8), in_=src.rearrange("p (g t) (c i) -> p g c t i", g=2, i=8)
                 )
 
+        def scalar_regroup(i):
+            e, d0, width = UNITS[i]
+            nc.scalar.copy(
+                out=group_tile(i)[:, 1, :, :].rearrange("p (c i) t -> p c t i", i=8),
+                in_=state["w", e][:, 4:8, d0:d0 + width].rearrange("p t (c i) -> p c t i", i=8),
+            )
+
         def unit_quant(i):
-            ww = cpool.tile([P, 2 * DH], U32, name="ww", tag="ww", align_bytes=64)
-            ws = cpool.tile([P, 2 * DH], U8, name="ws", tag="ws", align_bytes=64)
+            width = UNITS[i][2]
+            ww = cpool.tile([P, 2 * width], U32, name="ww", tag="ww", align_bytes=64)
+            ws = cpool.tile([P, 2 * width], U8, name="ws", tag="ws", align_bytes=64)
             nc.vector.quantize_mx(out=ww[:].bitcast(FP8X4), scales=ws[:], in_=state["wg", i][:].rearrange("p g d t -> p (g d t)"))
             state["codes", i] = (ww, ws)
 
         def unit_mm(i):
-            eg, el = divmod(UNITS[i][0], 4)
+            e, d0, width = UNITS[i]
+            eg, el = divmod(e, 4)
             ww, ws = state["codes", i]
             ps1 = psum.tile([P, 4, P], F32, name="ps1", tag="ps1")
-            for dl in range(2):
+            for dl in range(width // P):
                 for g in range(2):
-                    c0 = g * DH + dl * P
+                    c0 = g * width + dl * P
                     a = 4 * g + el
                     nc.tensor.matmul_mx(
                         out=ps1[:, dl, :],
@@ -141,20 +147,19 @@ def tile_softmoe_pb_kernel(tc, h, w2, b2, logits, out):
                     )
             state["ps1", i] = ps1
 
-        def unit_out(i):
-            e, dh = UNITS[i]
-            for dl in range(2):
-                dc = 2 * dh + dl
-                nc.scalar.activation(
-                    out=eoT[:, dc, :, NS * e:NS * (e + 1)],
-                    in_=state["ps1", i][:, dl, :].rearrange("p (b s) -> p b s", b=NB),
-                    func=ACT.Identity,
-                    bias=b2T[:, dc, e:e + 1],
-                    scale=1.0,
-                )
+        def unit_out(i, on_vector=False):
+            e, d0, width = UNITS[i]
+            for dl in range(width // P):
+                dc = d0 // P + dl
+                dst = eoT[:, dc, :, NS * e:NS * (e + 1)]
+                src = state["ps1", i][:, dl, :].rearrange("p (b s) -> p b s", b=NB)
+                if on_vector:
+                    nc.vector.tensor_scalar(out=dst, in0=src, scalar1=b2T[:, dc, e:e + 1], scalar2=None, op0=ALU.add)
+                else:
+                    nc.scalar.activation(out=dst, in_=src, func=ACT.Identity, bias=b2T[:, dc, e:e + 1], scale=1.0)
 
         def sm_max(b):
-            x = lraw[b]
+            x = lraw[b // 2][:, 4 * (b % 2):4 * (b % 2) + 4, :]
             m1 = smpool.tile([P, 4, 256], BF16, name="m1", tag="m1", bufs=1)
             nc.vector.tensor_tensor(out=m1[:], in0=x[:, :, 0:256], in1=x[:, :, 256:512], op=ALU.max)
             m2 = smpool.tile([P, 4, 128], BF16, name="m2", tag="m2", bufs=1)
@@ -169,7 +174,7 @@ def tile_softmoe_pb_kernel(tc, h, w2, b2, logits, out):
         def sm_exp(b, j):
             ef = epool.tile([P, 512], F32, name="ef", tag="ef")
             nc.scalar.activation(
-                out=ef[:], in_=lraw[b][:, j, :], func=ACT.Exp,
+                out=ef[:], in_=lraw[b // 2][:, 4 * (b % 2) + j, :], func=ACT.Exp,
                 bias=state["nmax", b][:, j:j + 1], scale=1.0, accum_out=state["ssum", b][:, j:j + 1],
             )
             state["ef", b, j] = ef
@@ -199,36 +204,46 @@ def tile_softmoe_pb_kernel(tc, h, w2, b2, logits, out):
                 out=cw_words[b][:].bitcast(FP8X4), scales=cw_scales[b][:], in_=state["gc", b][:].rearrange("p j l t -> p (j l t)")
             )
 
-        def eo_tr(b, dh):
-            tps = psum.tile([P, 2, DH], F32, name="tps", tag=("tr", "tr", "ps1", "ps1")[b] if dh == 1 else "tr")
-            for dl in range(2):
-                pairs = eoT[:, 2 * dh + dl, b, :].bitcast(F32)
-                for u in range(2):
-                    nc.tensor.transpose(tps[:, u, dl * P:(dl + 1) * P], pairs[:, u * P:(u + 1) * P], ident_f[:])
-            state["tps", b] = tps
+        def eo_tr(part, n, tag):
+            d0, width = PARTS[part]
+            nb = DH // width
+            tps = psum.tile([P, nb, 2, width], F32, name="tps", tag=tag)
+            for r in range(nb):
+                for dl in range(width // P):
+                    pairs = eoT[:, d0 // P + dl, nb * n + r, :].bitcast(F32)
+                    for u in range(2):
+                        nc.tensor.transpose(tps[:, r, u, dl * P:(dl + 1) * P], pairs[:, u * P:(u + 1) * P], ident_f[:])
+            state["tps", part, n] = tps
 
-        def eo_out(b, dh, on_vector):
-            if dh == 0:
-                state["eo", b] = shared.tile([P, ND, 4], BF16, name="eo", tag="big", align_bytes=64)
-            dst = state["eo", b][:, DH * dh:DH * (dh + 1), :].bitcast(F32)
-            src = state["tps", b][:].rearrange("p u d -> p d u")
+        def eo_out(part, n, on_vector):
+            d0, width = PARTS[part]
+            nb = DH // width
+            q, r = divmod(nb * n, 2)
+            if part == 0 and r == 0:
+                state["eo", q] = shared.tile([P, 2, ND, 4], BF16, name="eo", tag="big", align_bytes=64)
+            dst = state["eo", q][:, r:r + nb, d0:d0 + width, :].bitcast(F32)
+            src = state["tps", part, n][:].rearrange("p b u d -> p b d u")
             if on_vector:
                 nc.vector.tensor_copy(out=dst, in_=src)
             else:
                 nc.scalar.copy(out=dst, in_=src)
 
-        def eo_quant(b, dh):
-            cols = slice(DH * dh, DH * (dh + 1))
+        def eo_quant(part, b):
+            d0, width = PARTS[part]
+            cols = slice(d0, d0 + width)
             nc.vector.quantize_mx(
-                out=eo_words[b][:, cols].bitcast(FP8X4), scales=eo_scales[b][:, cols], in_=state["eo", b][:, cols, :].rearrange("p d t -> p (d t)")
+                out=eo_words[b][:, cols].bitcast(FP8X4), scales=eo_scales[b][:, cols],
+                in_=state["eo", b // 2][:, b % 2, cols, :].rearrange("p d t -> p (d t)"),
             )
 
-        def combine_mm(b, dh):
-            cols = slice(DH * dh, DH * (dh + 1))
-            for jp in range(2):
-                ps2 = psum.tile([P, 2, DH], F32, name="ps2", tag=("ps2", "cps")[jp])
-                for jj in range(2):
-                    j = 2 * jp + jj
+        def combine_mm(part, b):
+            d0, width = PARTS[part]
+            cols = slice(d0, d0 + width)
+            nj = 512 // width
+            for k in range(4 // nj):
+                ps2 = psum.tile([P, nj, width], F32, name="ps2", tag=("ps2", "cps")[k if nj == 2 else b % 2])
+                for jj in range(nj):
+                    j = nj * k + jj
                     nc.tensor.matmul_mx(
                         out=ps2[:, jj, :],
                         lhsT=cw_words[b][:, j * P:(j + 1) * P].bitcast(FP8X4),
@@ -238,16 +253,18 @@ def tile_softmoe_pb_kernel(tc, h, w2, b2, logits, out):
                         start=True,
                         stop=True,
                     )
-                state["ps2", b, jp] = ps2
+                state["ps2", part, b, k] = ps2
 
-        def combine_out(b, dh, jp, on_vector):
-            ob = opool.tile([P, 2, DH], F32, name="ob", tag="ob")
+        def combine_out(part, b, k, on_vector):
+            d0, width = PARTS[part]
+            nj = 512 // width
+            ob = opool.tile([P, nj, width], F32, name="ob", tag="ob")
             if on_vector:
-                nc.vector.tensor_copy(out=ob[:], in_=state["ps2", b, jp][:])
+                nc.vector.tensor_copy(out=ob[:], in_=state["ps2", part, b, k][:])
             else:
-                nc.scalar.copy(out=ob[:], in_=state["ps2", b, jp][:])
+                nc.scalar.copy(out=ob[:], in_=state["ps2", part, b, k][:])
             dram = out[b].rearrange("(p j) d -> p j d", j=4)
-            nc.sync.dma_start(out=dram[:, 2 * jp:2 * jp + 2, DH * dh:DH * (dh + 1)], in_=ob[:])
+            nc.sync.dma_start(out=dram[:, nj * k:nj * (k + 1), d0:d0 + width], in_=ob[:])
 
         def bias():
             bps = psum.tile([P, 4, P], BF16, name="bps", tag="ps2")
@@ -286,17 +303,20 @@ def tile_softmoe_pb_kernel(tc, h, w2, b2, logits, out):
                 at(s0 + b + 1, h_out, eg, b)
             at(s0 + 7, h_quant, eg)
         for b in range(NB):
-            at(26 + b, eo_out, b, 0, False)
-            at(27 + b, eo_quant, b, 0)
-            at(27 + b, combine_mm, b, 0)
-            for jp in range(2):
-                if b < 3:
-                    at(28 + b, combine_out, b, 0, jp, False)
-        loads = {2: [(load_w, 4), (load_h, 2), (load_w, 5), (load_logits, 2), (load_w, 6)], 6: [(load_w, 7), (load_h, 3), (load_w, 8), (load_w, 9)],
-                 7: [(load_w, 10), (load_logits, 3)]}
+            at(26 + 2 * b, eo_out, 0, b, False)
+            at(28 + 2 * b, eo_quant, 0, b)
+            at(28 + 2 * b, combine_mm, 0, b)
+            for k in range(2):
+                at(29 + 2 * b + k, combine_out, 0, b, k, False)
+        for q in range(2):
+            at(35 + 2 * q, eo_out, 1, q, False)
+            for b in (2 * q, 2 * q + 1):
+                at(37 + 2 * q, eo_quant, 1, b)
+                at(37 + 2 * q, combine_mm, 1, b)
+        loads = {2: [(load_w, 4), (load_h, 2), (load_w, 5), (load_logits, 2), (load_w, 6)], 6: [(load_w, 7), (load_h, 3), (load_w, 8), (load_logits, 3), (load_w, 9)],
+                 7: [(load_w, 10)]}
         for e in range(11, NE):
             loads[2 * (e - E_SPLIT) + 2] = [(load_w, e)]
-
         with tc.manual_schedule():
             nc.vector.memset(zero[:], 0.0)
             nc.scalar.activation(out=warm[:], in_=zero[:], func=ACT.Exp)
@@ -305,18 +325,20 @@ def tile_softmoe_pb_kernel(tc, h, w2, b2, logits, out):
                              (load_h, (1,)), (load_w, (3,)), (sm_max, (0,))):
                 fn(*args)
             for s in range(NU + 2):
-                if s + S_AHEAD in ON_SCALAR:
-                    regroup(s + S_AHEAD, True)
+                if s + 1 in ON_SCALAR:
+                    scalar_regroup(s + 1)
                 if s < NU:
-                    regroup(s, False)
+                    regroup(s)
                 for fn, args in loads.get(s, []):
                     fn(args)
                 for fn, args in extras.get(s, []):
                     fn(*args)
                 if s >= 5:
-                    unit_out(s - 2)
-                if 25 <= s < 25 + NB:
-                    eo_tr(s - 25, 0)
+                    unit_out(s - 2, s == NU + 1)
+                if 25 <= s < 25 + 2 * NB and s % 2 == 1:
+                    eo_tr(0, (s - 25) // 2, "tr")
+                if s in (34, 36):
+                    eo_tr(1, (s - 34) // 2, "tr")
                 if 1 <= s <= NU:
                     unit_quant(s - 1)
                 if s == 4:
@@ -329,16 +351,15 @@ def tile_softmoe_pb_kernel(tc, h, w2, b2, logits, out):
                     unit_out(2)
                 elif 5 <= s <= NU:
                     unit_mm(s - 1)
-            for jp in range(2):
-                combine_out(3, 0, jp, True)
+            for q in range(2):
+                eo_tr(2, q, "ps1")
             for b in range(NB):
-                eo_tr(b, 1)
-            for k in range(NB + 2):
-                if k < NB:
-                    eo_out(k, 1, k == 1)
-                if 1 <= k <= NB:
-                    eo_quant(k - 1, 1)
-                    combine_mm(k - 1, 1)
-                if k >= 2:
-                    combine_out(k - 2, 1, 0, True)
-                    combine_out(k - 2, 1, 1, False)
+                combine_out(1, b, 0, b < 2)
+            for q in range(2):
+                eo_out(2, q, q == 1)
+            for b in range(NB):
+                eo_quant(2, b)
+                combine_mm(2, b)
+                if b > 0:
+                    combine_out(2, b - 1, 0, b % 2 == 1)
+            combine_out(2, 3, 0, False)

@@ -21,7 +21,7 @@ E_SPLIT = 8
 PARTS = ((0, 256), (256, 128), (384, 128))
 UNITS = [(e, d0, DH) for e in range(E_SPLIT) for d0 in (0, DH)] + [(e, d0, width) for d0, width in PARTS for e in range(E_SPLIT, NE)]
 NU = len(UNITS)
-ON_SCALAR = (8, 11, 14, 17, 20)
+ON_SCALAR = (11, 14, 17, 20, 23)
 
 
 def tile_softmoe_pb_kernel(tc, h, w2, b2, logits, out):
@@ -33,9 +33,9 @@ def tile_softmoe_pb_kernel(tc, h, w2, b2, logits, out):
         epool = ctx.enter_context(tc.tile_pool(name="epool", bufs=4))
         hpool = ctx.enter_context(tc.tile_pool(name="hpool", bufs=2))
         wpool = ctx.enter_context(tc.tile_pool(name="wpool", bufs=8))
-        gpool = ctx.enter_context(tc.tile_pool(name="gpool", bufs=4))
-        cpool = ctx.enter_context(tc.tile_pool(name="cpool", bufs=4))
-        opool = ctx.enter_context(tc.tile_pool(name="opool", bufs=8))
+        gpool = ctx.enter_context(tc.tile_pool(name="gpool", bufs=5))
+        cpool = ctx.enter_context(tc.tile_pool(name="cpool", bufs=5))
+        opool = ctx.enter_context(tc.tile_pool(name="opool", bufs=6))
         psum = ctx.enter_context(tc.psum_pool(name="psum", bufs=2))
 
         zero = const.tile([P, 1], F32, name="zero")
@@ -58,8 +58,8 @@ def tile_softmoe_pb_kernel(tc, h, w2, b2, logits, out):
 
         def load_w(e):
             wraw = wpool.tile([P, 8, ND], BF16, name="wraw", tag="wraw")
-            src = w2[e].rearrange("(c p r) d -> p c (r d)", c=4, p=P, r=2)
-            nc.sync.dma_start(out=wraw[:].rearrange("p (c r) d -> p c (r d)", c=4, r=2), in_=src)
+            src = w2[e].rearrange("(g p t) d -> p g (t d)", g=2, p=P, t=4)
+            nc.sync.dma_start(out=wraw[:].rearrange("p (g t) d -> p g (t d)", g=2, t=4), in_=src)
             state["w", e] = wraw
 
         def load_h(eg):
@@ -82,9 +82,8 @@ def tile_softmoe_pb_kernel(tc, h, w2, b2, logits, out):
             words = state["h", eg][:, b, :].bitcast(F32)
             for g in range(2):
                 for u in range(2):
-                    c = 2 * g + u
                     nc.tensor.transpose(
-                        hps[:, u, 4 * g:4 * g + 4, :].rearrange("p e s -> p (e s)"), words[:, c * P:(c + 1) * P], ident_f[:]
+                        hps[:, u, 4 * g:4 * g + 4, :].rearrange("p e s -> p (e s)"), words[:, 256 * g + u:256 * (g + 1):2], ident_f[:]
                     )
             state["hps", eg, b] = hps
 
@@ -287,7 +286,7 @@ def tile_softmoe_pb_kernel(tc, h, w2, b2, logits, out):
                 at(s0 + 5 + j // 2, sm_tr, b, j)
             at(s0 + 6, sm_out, b, 0)
             at(s0 + 7, sm_out, b, 1)
-            at(s0 + 9, sm_quant, b)
+            at(s0 + 11, sm_quant, b)
         at(1, sm_max, 1)
         at(0, bias)
         for b in range(2):
@@ -316,7 +315,7 @@ def tile_softmoe_pb_kernel(tc, h, w2, b2, logits, out):
         loads = {2: [(load_w, 4), (load_h, 2), (load_w, 5), (load_logits, 2), (load_w, 6)], 6: [(load_w, 7), (load_h, 3), (load_w, 8), (load_logits, 3), (load_w, 9)],
                  7: [(load_w, 10)]}
         for e in range(11, NE):
-            loads[2 * (e - E_SPLIT) + 2] = [(load_w, e)]
+            loads[2 * (e - 8) + 2] = [(load_w, e)]
         with tc.manual_schedule():
             nc.vector.memset(zero[:], 0.0)
             nc.scalar.activation(out=warm[:], in_=zero[:], func=ACT.Exp)
@@ -335,7 +334,7 @@ def tile_softmoe_pb_kernel(tc, h, w2, b2, logits, out):
                     fn(*args)
                 if s >= 5:
                     unit_out(s - 2, s == NU + 1)
-                if 25 <= s < 25 + 2 * NB and s % 2 == 1:
+                if 25 <= s < 25 + 2 * NB and (s - 25) % 2 == 0:
                     eo_tr(0, (s - 25) // 2, "tr")
                 if s in (34, 36):
                     eo_tr(1, (s - 34) // 2, "tr")

from contextlib import ExitStack

import concourse.mybir as mybir
from concourse.masks import make_identity

F32 = mybir.dt.float32
BF16 = mybir.dt.bfloat16
U32 = mybir.dt.uint32
U8 = mybir.dt.uint8
FP8X4 = mybir.dt.float8_e4m3fn_x4
ACT = mybir.ActivationFunctionType
ALU = mybir.AluOpType
AXIS = mybir.AxisListType

P = 128
NB, NL, ND, NE, NS, NH = 4, 512, 512, 16, 32, 1024
FLOPS = 2 * NB * NE * NS * NH * ND + 2 * NB * NL * NE * NS * ND
DH = 256

E_SPLIT = 8
PARTS = ((0, 256), (256, 128), (384, 128))
UNITS = [(e, d0, DH) for e in range(E_SPLIT) for d0 in (0, DH)] + [(e, d0, width) for d0, width in PARTS for e in range(E_SPLIT, NE)]
NU = len(UNITS)
ON_SCALAR = (11, 14, 17, 20, 23)


def tile_softmoe_pb_kernel(tc, h, w2, b2, logits, out):
    nc = tc.nc
    with ExitStack() as ctx:
        const = ctx.enter_context(tc.tile_pool(name="const", bufs=1))
        shared = ctx.enter_context(tc.tile_pool(name="shared", bufs=2))
        smpool = ctx.enter_context(tc.tile_pool(name="smpool", bufs=2))
        epool = ctx.enter_context(tc.tile_pool(name="epool", bufs=4))
        hpool = ctx.enter_context(tc.tile_pool(name="hpool", bufs=2))
        wpool = ctx.enter_context(tc.tile_pool(name="wpool", bufs=8))
        gpool = ctx.enter_context(tc.tile_pool(name="gpool", bufs=5))
        cpool = ctx.enter_context(tc.tile_pool(name="cpool", bufs=5))
        opool = ctx.enter_context(tc.tile_pool(name="opool", bufs=6))
        psum = ctx.enter_context(tc.psum_pool(name="psum", bufs=2))

        zero = const.tile([P, 1], F32, name="zero")
        warm = const.tile([P, 1], F32, name="warm")
        ident_f = const.tile([P, P], F32, name="ident_f")
        make_identity(nc, ident_f[:])
        ident_b = const.tile([P, P], BF16, name="ident_b")
        make_identity(nc, ident_b[:])
        h_words = [const.tile([P, 1024], U32, name="h_words%d" % eg, align_bytes=64) for eg in range(4)]
        h_scales = [const.tile([P, 1024], U8, name="h_scales%d" % eg, align_bytes=64) for eg in range(4)]
        cw_words = [const.tile([P, NL], U32, name="cw_words%d" % b, align_bytes=64) for b in range(NB)]
        cw_scales = [const.tile([P, NL], U8, name="cw_scales%d" % b, align_bytes=64) for b in range(NB)]
        eo_words = [const.tile([P, ND], U32, name="eo_words%d" % b, align_bytes=64) for b in range(NB)]
        eo_scales = [const.tile([P, ND], U8, name="eo_scales%d" % b, align_bytes=64) for b in range(NB)]
        lraw = [shared.tile([P, 8, 512], BF16, name="lraw%d" % q, tag="big", align_bytes=64) for q in range(2)]
        eoT = const.tile([P, 4, NB, 512], BF16, name="eoT")
        b2z = const.tile([P, ND], BF16, name="b2z")
        b2T = const.tile([P, 4, NE], F32, name="b2T")
        state = {}

        def load_w(e):
            wraw = wpool.tile([P, 8, ND], BF16, name="wraw", tag="wraw")
            src = w2[e].rearrange("(g p t) d -> p g (t d)", g=2, p=P, t=4)
            nc.sync.dma_start(out=wraw[:].rearrange("p (g t) d -> p g (t d)", g=2, t=4), in_=src)
            state["w", e] = wraw

        def load_h(eg):
            hraw = hpool.tile([P, NB, NH], BF16, name="hraw", tag="hraw")
            for b in range(NB):
                nc.sync.dma_start(out=hraw[:, b, :], in_=h[b, 4 * eg:4 * eg + 4].rearrange("e s k -> (e s) k"))
            state["h", eg] = hraw

        def load_b2():
            nc.sync.dma_start(out=b2z[0:NE, :], in_=b2)

        def load_logits(b):
            q, r = divmod(b, 2)
            nc.sync.dma_start(out=lraw[q][:, 4 * r:4 * r + 4, :], in_=logits[b].rearrange("(p j) e s -> p j (e s)", j=4))

        def h_tr(eg, b):
            if b == 0:
                state["gh", eg] = hpool.tile([P, 4096], BF16, name="gh", tag="gh", align_bytes=64)
            hps = psum.tile([P, 2, 8, NS], F32, name="hps", tag="tr")
            words = state["h", eg][:, b, :].bitcast(F32)
            for g in range(2):
                for u in range(2):
                    nc.tensor.transpose(
                        hps[:, u, 4 * g:4 * g + 4, :].rearrange("p e s -> p (e s)"), words[:, 256 * g + u:256 * (g + 1):2], ident_f[:]
                    )
            state["hps", eg, b] = hps

        def h_out(eg, b):
            gh32 = state["gh", eg][:].bitcast(F32).rearrange("p (a b s u) -> p a b s u", a=8, b=NB, s=NS, u=2)
            nc.scalar.copy(out=gh32[:, :, b, :, :], in_=state["hps", eg, b][:].rearrange("p u a s -> p a s u"))

        def h_quant(eg):
            nc.vector.quantize_mx(out=h_words[eg][:].bitcast(FP8X4), scales=h_scales[eg][:], in_=state["gh", eg][:])

        def group_tile(i):
            if ("wg", i) not in state:
                state["wg", i] = gpool.tile([P, 2, UNITS[i][2], 4], BF16, name="wg", tag="wg", align_bytes=64)
            return state["wg", i]

        def regroup(i):
            e, d0, width = UNITS[i]
            wg = group_tile(i)
            src = state["w", e][:, :, d0:d0 + width]
            if i in ON_SCALAR:
                nc.vector.tensor_copy(
                    out=wg[:, 0, :, :].rearrange("p (c i) t -> p c t i", i=8), in_=src[:, 0:4, :].rearrange("p t (c i) -> p c t i", i=8)
                )
            else:
                nc.vector.tensor_copy(
                    out=wg[:].rearrange("p g (c i) t -> p g c t i", i=8), in_=src.rearrange("p (g t) (c i) -> p g c t i", g=2, i=8)
                )

        def scalar_regroup(i):
            e, d0, width = UNITS[i]
            nc.scalar.copy(
                out=group_tile(i)[:, 1, :, :].rearrange("p (c i) t -> p c t i", i=8),
                in_=state["w", e][:, 4:8, d0:d0 + width].rearrange("p t (c i) -> p c t i", i=8),
            )

        def unit_quant(i):
            width = UNITS[i][2]
            ww = cpool.tile([P, 2 * width], U32, name="ww", tag="ww", align_bytes=64)
            ws = cpool.tile([P, 2 * width], U8, name="ws", tag="ws", align_bytes=64)
            nc.vector.quantize_mx(out=ww[:].bitcast(FP8X4), scales=ws[:], in_=state["wg", i][:].rearrange("p g d t -> p (g d t)"))
            state["codes", i] = (ww, ws)

        def unit_mm(i):
            e, d0, width = UNITS[i]
            eg, el = divmod(e, 4)
            ww, ws = state["codes", i]
            ps1 = psum.tile([P, 4, P], F32, name="ps1", tag="ps1")
            for dl in range(width // P):
                for g in range(2):
                    c0 = g * width + dl * P
                    a = 4 * g + el
                    nc.tensor.matmul_mx(
                        out=ps1[:, dl, :],
                        lhsT=ww[:, c0:c0 + P].bitcast(FP8X4),
                        lhsT_scale=ws[:, c0:c0 + P],
                        rhs=h_words[eg][:, a * P:(a + 1) * P].bitcast(FP8X4),
                        rhs_scale=h_scales[eg][:, a * P:(a + 1) * P],
                        start=(g == 0),
                        stop=(g == 1),
                    )
            state["ps1", i] = ps1

        def unit_out(i, on_vector=False):
            e, d0, width = UNITS[i]
            for dl in range(width // P):
                dc = d0 // P + dl
                dst = eoT[:, dc, :, NS * e:NS * (e + 1)]
                src = state["ps1", i][:, dl, :].rearrange("p (b s) -> p b s", b=NB)
                if on_vector:
                    nc.vector.tensor_scalar(out=dst, in0=src, scalar1=b2T[:, dc, e:e + 1], scalar2=None, op0=ALU.add)
                else:
                    nc.scalar.activation(out=dst, in_=src, func=ACT.Identity, bias=b2T[:, dc, e:e + 1], scale=1.0)

        def sm_max(b):
            x = lraw[b // 2][:, 4 * (b % 2):4 * (b % 2) + 4, :]
            m1 = smpool.tile([P, 4, 256], BF16, name="m1", tag="m1", bufs=1)
            nc.vector.tensor_tensor(out=m1[:], in0=x[:, :, 0:256], in1=x[:, :, 256:512], op=ALU.max)
            m2 = smpool.tile([P, 4, 128], BF16, name="m2", tag="m2", bufs=1)
            nc.vector.tensor_tensor(out=m2[:], in0=m1[:, :, 0:128], in1=m1[:, :, 128:256], op=ALU.max)
            mx = smpool.tile([P, 4], F32, name="mx", tag="mx")
            nc.vector.tensor_reduce(out=mx[:], in_=m2[:], axis=AXIS.X, op=ALU.max)
            nmax = smpool.tile([P, 4], F32, name="nmax", tag="nmax")
            nc.vector.tensor_scalar(out=nmax[:], in0=mx[:], scalar1=-1.0, scalar2=None, op0=ALU.mult)
            state["nmax", b] = nmax
            state["ssum", b] = smpool.tile([P, 4], F32, name="ssum", tag="ssum")

        def sm_exp(b, j):
            ef = epool.tile([P, 512], F32, name="ef", tag="ef")
            nc.scalar.activation(
                out=ef[:], in_=lraw[b // 2][:, 4 * (b % 2) + j, :], func=ACT.Exp,
                bias=state["nmax", b][:, j:j + 1], scale=1.0, accum_out=state["ssum", b][:, j:j + 1],
            )
            state["ef", b, j] = ef

        def sm_norm(b):
            rinv = smpool.tile([P, 4], F32, name="rinv", tag="rinv")
            nc.vector.reciprocal(out=rinv[:], in_=state["ssum", b][:])
            state["rinv", b] = rinv
            state["gc", b] = smpool.tile([P, 4, P, 4], BF16, name="gc", tag="gc", align_bytes=64)

        def sm_tr(b, j):
            cw = epool.tile([P, 512], BF16, name="cw", tag="cw")
            nc.scalar.activation(out=cw[:], in_=state["ef", b, j][:], func=ACT.Copy, scale=state["rinv", b][:, j:j + 1])
            if j % 2 == 0:
                state["cps", b, j // 2] = psum.tile([P, 2, 2, P], F32, name="cps", tag="cps")
            pairs = cw[:].bitcast(F32)
            for u in range(2):
                nc.tensor.transpose(state["cps", b, j // 2][:, j % 2, u, :], pairs[:, u * P:(u + 1) * P], ident_f[:])

        def sm_out(b, jp):
            nc.scalar.copy(
                out=state["gc", b][:, 2 * jp:2 * jp + 2, :, :].bitcast(F32), in_=state["cps", b, jp][:].rearrange("p j u l -> p j l u")
            )

        def sm_quant(b):
            nc.vector.quantize_mx(
                out=cw_words[b][:].bitcast(FP8X4), scales=cw_scales[b][:], in_=state["gc", b][:].rearrange("p j l t -> p (j l t)")
            )

        def eo_tr(part, n, tag):
            d0, width = PARTS[part]
            nb = DH // width
            tps = psum.tile([P, nb, 2, width], F32, name="tps", tag=tag)
            for r in range(nb):
                for dl in range(width // P):
                    pairs = eoT[:, d0 // P + dl, nb * n + r, :].bitcast(F32)
                    for u in range(2):
                        nc.tensor.transpose(tps[:, r, u, dl * P:(dl + 1) * P], pairs[:, u * P:(u + 1) * P], ident_f[:])
            state["tps", part, n] = tps

        def eo_out(part, n, on_vector):
            d0, width = PARTS[part]
            nb = DH // width
            q, r = divmod(nb * n, 2)
            if part == 0 and r == 0:
                state["eo", q] = shared.tile([P, 2, ND, 4], BF16, name="eo", tag="big", align_bytes=64)
            dst = state["eo", q][:, r:r + nb, d0:d0 + width, :].bitcast(F32)
            src = state["tps", part, n][:].rearrange("p b u d -> p b d u")
            if on_vector:
                nc.vector.tensor_copy(out=dst, in_=src)
            else:
                nc.scalar.copy(out=dst, in_=src)

        def eo_quant(part, b):
            d0, width = PARTS[part]
            cols = slice(d0, d0 + width)
            nc.vector.quantize_mx(
                out=eo_words[b][:, cols].bitcast(FP8X4), scales=eo_scales[b][:, cols],
                in_=state["eo", b // 2][:, b % 2, cols, :].rearrange("p d t -> p (d t)"),
            )

        def combine_mm(part, b):
            d0, width = PARTS[part]
            cols = slice(d0, d0 + width)
            nj = 512 // width
            for k in range(4 // nj):
                ps2 = psum.tile([P, nj, width], F32, name="ps2", tag=("ps2", "cps")[k if nj == 2 else b % 2])
                for jj in range(nj):
                    j = nj * k + jj
                    nc.tensor.matmul_mx(
                        out=ps2[:, jj, :],
                        lhsT=cw_words[b][:, j * P:(j + 1) * P].bitcast(FP8X4),
                        lhsT_scale=cw_scales[b][:, j * P:(j + 1) * P],
                        rhs=eo_words[b][:, cols].bitcast(FP8X4),
                        rhs_scale=eo_scales[b][:, cols],
                        start=True,
                        stop=True,
                    )
                state["ps2", part, b, k] = ps2

        def combine_out(part, b, k, on_vector):
            d0, width = PARTS[part]
            nj = 512 // width
            ob = opool.tile([P, nj, width], F32, name="ob", tag="ob")
            if on_vector:
                nc.vector.tensor_copy(out=ob[:], in_=state["ps2", part, b, k][:])
            else:
                nc.scalar.copy(out=ob[:], in_=state["ps2", part, b, k][:])
            dram = out[b].rearrange("(p j) d -> p j d", j=4)
            nc.sync.dma_start(out=dram[:, nj * k:nj * (k + 1), d0:d0 + width], in_=ob[:])

        def bias():
            bps = psum.tile([P, 4, P], BF16, name="bps", tag="ps2")
            for dc in range(4):
                nc.tensor.transpose(bps[:, dc, :], b2z[:, dc * P:(dc + 1) * P], ident_b[:])
            nc.vector.tensor_copy(out=b2T[:], in_=bps[:, :, 0:NE])

        extras = {}

        def at(slot, fn, *args):
            extras[slot] = extras.get(slot, []) + [(fn, args)]

        for b, s0 in enumerate((-2, 5, 11, 17)):
            if b > 1:
                at(s0, sm_max, b)
            for j in range(4):
                at(max(s0 + 1 + j, 0) if b else 0, sm_exp, b, j)
            at(s0 + 5, sm_norm, b)
            for j in range(4):
                at(s0 + 5 + j // 2, sm_tr, b, j)
            at(s0 + 6, sm_out, b, 0)
            at(s0 + 7, sm_out, b, 1)
            at(s0 + 11, sm_quant, b)
        at(1, sm_max, 1)
        at(0, bias)
        for b in range(2):
            at(0, h_tr, 0, b)
            at(1, h_out, 0, b)
        for b in range(2, 4):
            at(1, h_tr, 0, b)
            at(2, h_out, 0, b)
        at(4, h_quant, 0)
        for eg, s0 in ((1, 2), (2, 6), (3, 12)):
            for b in range(NB):
                at(s0 + b, h_tr, eg, b)
                at(s0 + b + 1, h_out, eg, b)
            at(s0 + 7, h_quant, eg)
        for b in range(NB):
            at(26 + 2 * b, eo_out, 0, b, False)
            at(28 + 2 * b, eo_quant, 0, b)
            at(28 + 2 * b, combine_mm, 0, b)
            for k in range(2):
                at(29 + 2 * b + k, combine_out, 0, b, k, False)
        for q in range(2):
            at(35 + 2 * q, eo_out, 1, q, False)
            for b in (2 * q, 2 * q + 1):
                at(37 + 2 * q, eo_quant, 1, b)
                at(37 + 2 * q, combine_mm, 1, b)
        loads = {2: [(load_w, 4), (load_h, 2), (load_w, 5), (load_logits, 2), (load_w, 6)], 6: [(load_w, 7), (load_h, 3), (load_w, 8), (load_logits, 3), (load_w, 9)],
                 7: [(load_w, 10)]}
        for e in range(11, NE):
            loads[2 * (e - 8) + 2] = [(load_w, e)]
        with tc.manual_schedule():
            nc.vector.memset(zero[:], 0.0)
            nc.scalar.activation(out=warm[:], in_=zero[:], func=ACT.Exp)
            nc.vector.memset(b2z[:], 0.0)
            for fn, args in ((load_logits, (0,)), (load_b2, ()), (load_w, (0,)), (load_logits, (1,)), (load_w, (1,)), (load_h, (0,)), (load_w, (2,)),
                             (load_h, (1,)), (load_w, (3,)), (sm_max, (0,))):
                fn(*args)
            for s in range(NU + 2):
                if s + 1 in ON_SCALAR:
                    scalar_regroup(s + 1)
                if s < NU:
                    regroup(s)
                for fn, args in loads.get(s, []):
                    fn(args)
                for fn, args in extras.get(s, []):
                    fn(*args)
                if s >= 5:
                    unit_out(s - 2, s == NU + 1)
                if 25 <= s < 25 + 2 * NB and (s - 25) % 2 == 0:
                    eo_tr(0, (s - 25) // 2, "tr")
                if s in (34, 36):
                    eo_tr(1, (s - 34) // 2, "tr")
                if 1 <= s <= NU:
                    unit_quant(s - 1)
                if s == 4:
                    unit_mm(0)
                    unit_mm(1)
                    unit_out(0)
                    unit_mm(2)
                    unit_out(1)
                    unit_mm(3)
                    unit_out(2)
                elif 5 <= s <= NU:
                    unit_mm(s - 1)
            for q in range(2):
                eo_tr(2, q, "ps1")
            for b in range(NB):
                combine_out(1, b, 0, b < 2)
            for q in range(2):
                eo_out(2, q, q == 1)
            for b in range(NB):
                eo_quant(2, b)
                combine_mm(2, b)
                if b > 0:
                    combine_out(2, b - 1, 0, b % 2 == 1)
            combine_out(2, 3, 0, False)
